import numpy as np
import ml_dtypes


def mxq(x, axis, fmt="e4m3"):
    dtype, down = {"e4m3": (ml_dtypes.float8_e4m3fn, 7), "e5m2": (ml_dtypes.float8_e5m2, 14)}[fmt]
    v = np.moveaxis(np.asarray(x, np.float32).astype(ml_dtypes.bfloat16).astype(np.float64), axis, -1)
    blocks = v.reshape(v.shape[:-1] + (-1, 32))
    amax = np.abs(blocks).max(-1, keepdims=True)
    byte = np.maximum(np.where(amax > 0, np.frexp(amax)[1] - 1 + 127, 0) - down, 1)
    scale = np.exp2(byte - 127.0)
    codes = (blocks / scale).astype(np.float32).astype(dtype).astype(np.float64)
    return np.moveaxis((codes * scale).reshape(v.shape), -1, axis)


WIDE = False


def mx_kscale(k):
    if not WIDE:
        return np.ones(k)
    levels = np.array([10, -10, 5, -5, 0])
    if k % 512:
        return np.exp2(np.random.permutation(np.resize(levels, k // 32))).repeat(32)
    a = np.empty((k // 512, 16))
    for p in range(k // 512):
        a[p, :8] = np.random.permutation(np.resize(levels, 8))
        for g in range(8):
            far = levels[np.abs(levels - a[p, g]) >= 10]
            a[p, g + 8] = far[np.random.randint(len(far))]
    return np.exp2(a.ravel()).repeat(32)


BF16 = ml_dtypes.bfloat16


def bf(x):
    return np.asarray(x, np.float32).astype(BF16)


def f64(x):
    return np.asarray(x).astype(np.float64)


B, IN_F, N_HID = 4096, 768, 256
HEAD = N_HID + IN_F


def sigmoid(v):
    return 1.0 / (1.0 + np.exp(-v))


def setup_inputs():
    s = mx_kscale(HEAD)
    scale = 1.0 / np.sqrt(HEAD)
    raw = np.abs(np.random.randint(-1, 2, (IN_F, N_HID))).astype(np.float64)
    rec = (np.random.random((N_HID, N_HID)) < 0.9).astype(np.float64)
    mask = np.concatenate([raw, rec], axis=0).T

    def w():
        return bf(np.random.standard_normal((N_HID, HEAD)) * scale / s[None, :])

    def b():
        return bf(np.random.standard_normal(N_HID) * 0.3)

    return {
        "x": bf(np.random.standard_normal((B, IN_F)) * s[None, :IN_F]),
        "hidden": bf(np.random.standard_normal((B, N_HID)) * s[None, IN_F:]),
        "mask": bf(mask),
        "Wg": w(), "bg": b(),
        "Wh": w(), "bh": b(),
        "Wfg": w(), "bfg": b(),
        "Wfh": w(), "bfh": b(),
        "Wp": w(), "bp": b(),
    }


def reference(x, hidden, mask, Wg, bg, Wh, bh, Wfg, bfg, Wfh, bfh, Wp, bp):
    xc = np.concatenate([f64(x), f64(hidden)], axis=1)
    W_all = np.stack([f64(Wg), f64(Wh), f64(Wfg), f64(Wfh), f64(Wp)]) * f64(mask)[None]
    b_all = np.stack([f64(bg), f64(bh), f64(bfg), f64(bfh), f64(bp)])
    outs = (mxq(xc, 1, "e4m3") @ mxq(W_all, 2, "e4m3").transpose(0, 2, 1)) + b_all[:, None, :]
    g_out, h_out, fg_out, fh_out, p_out = outs
    g = np.tanh(g_out)
    h = np.tanh(h_out)
    gate = sigmoid(fg_out + fh_out)
    new_hidden = g * (1.0 - gate) + gate * h
    y_pred = p_out + new_hidden
    return (y_pred, new_hidden)

@@ -1,0 +1,689 @@
+from contextlib import ExitStack
+
+import concourse.mybir as mybir
+from concourse.masks import make_identity
+
+F32 = mybir.dt.float32
+BF16 = mybir.dt.bfloat16
+U32 = mybir.dt.uint32
+U8 = mybir.dt.uint8
+FP8X4 = mybir.dt.float8_e4m3fn_x4
+ALU = mybir.AluOpType
+ACT = mybir.ActivationFunctionType
+
+P = 128
+B, IN_F, N_HID = 4096, 768, 256
+K = IN_F + N_HID
+SB = 512
+JT = SB // P
+NSB = B // SB
+FLOPS = 2 * B * K * 5 * N_HID
+
+
+def tile_ncpliquidcell_t_kernel(
+    tc, x, hidden, mask, Wg, bg, Wh, bh, Wfg, bfg, Wfh, bfh, Wp, bp, out_0, out_1
+):
+    nc = tc.nc
+    weights = [Wg, Wh, Wfg, Wfh, Wp]
+    with ExitStack() as ctx:
+        const = ctx.enter_context(tc.tile_pool(name="const", bufs=1))
+        wraw = ctx.enter_context(tc.tile_pool(name="wraw", bufs=10))
+        wgr = ctx.enter_context(tc.tile_pool(name="wgr", bufs=2))
+        xin = ctx.enter_context(tc.tile_pool(name="xin", bufs=NSB))
+        xgr = ctx.enter_context(tc.tile_pool(name="xgr", bufs=2))
+        xq = ctx.enter_context(tc.tile_pool(name="xq", bufs=3))
+        act = ctx.enter_context(tc.tile_pool(name="act", bufs=3))
+        ep = ctx.enter_context(tc.tile_pool(name="ep", bufs=2))
+        outp = ctx.enter_context(tc.tile_pool(name="outp", bufs=3))
+        tr = ctx.enter_context(tc.psum_pool(name="tr", bufs=4))
+        mx = ctx.enter_context(tc.psum_pool(name="mx", bufs=4))
+        ctx.enter_context(tc.manual_schedule())
+
+        ones_bf = const.tile([P, P], BF16)
+        nc.vector.memset(ones_bf[:], 1.0)
+        dz = const.tile([P, 512], BF16)
+        nc.vector.memset(dz[:], 0.0)
+        zt_bf = const.tile([P, P], BF16)
+        nc.vector.memset(zt_bf[:], 0.0)
+        zb_bf = const.tile([P, N_HID], BF16)
+        nc.vector.memset(zb_bf[:], 0.0)
+        warm = const.tile([P, 1], F32)
+        nc.vector.memset(warm[:], 0.0)
+        warm2 = const.tile([P, 1], F32)
+        nc.scalar.activation(out=warm2[:], in_=warm[:], func=ACT.Tanh)
+        ident = const.tile([P, P], F32)
+        make_identity(nc, ident[:])
+        for i, b in enumerate([bg, bh, bfg, bfh]):
+            nc.gpsimd.dma_start(out=zt_bf[2 * i : 2 * i + 2, :], in_=b.rearrange("(r c) -> r c", r=2))
+        nc.gpsimd.dma_start(out=zb_bf[0:1, :], in_=bp.rearrange("(o c) -> o c", o=1))
+
+        mask_sb = [const.tile([P, K], BF16, name="mask%d" % hf) for hf in range(2)]
+        w_sb = [[wraw.tile([P, K], BF16, name="w%d_%d" % (w, hf), tag="w") for hf in range(2)] for w in range(5)]
+        x_sb = [xin.tile([P, JT, K], BF16, name="x%d" % s, tag="x") for s in range(NSB)]
+
+        def load_m(hf):
+            nc.sync.dma_start(out=mask_sb[hf][:], in_=mask[P * hf : P * (hf + 1), :])
+
+        def load_w(w, hf):
+            nc.sync.dma_start(out=w_sb[w][hf][:], in_=weights[w][P * hf : P * (hf + 1), :])
+
+        def load_x(s):
+            rows = slice(SB * s, SB * (s + 1))
+            nc.sync.dma_start(out=x_sb[s][:, :, 0:IN_F], in_=x[rows, :].rearrange("(p j) k -> p j k", j=JT))
+            nc.sync.dma_start(out=x_sb[s][:, :, IN_F:K], in_=hidden[rows, :].rearrange("(p j) k -> p j k", j=JT))
+
+        load_x(0)
+        load_m(0)
+        load_w(0, 0)
+        load_m(1)
+        load_w(0, 1)
+        load_w(1, 0)
+        load_w(1, 1)
+        load_x(1)
+        load_w(2, 0)
+        load_w(2, 1)
+        load_w(3, 0)
+        load_w(3, 1)
+        load_w(4, 0)
+        load_w(4, 1)
+        load_x(2)
+        load_x(3)
+        load_x(4)
+        load_x(5)
+        load_x(6)
+        load_x(7)
+
+        zt = const.tile([P, P], F32)
+        bias_sb = const.tile([P, 8], F32)
+        bf_sum = const.tile([P, 2], F32)
+        bf_half = const.tile([P, 2], F32)
+        bp_bc = const.tile([P, 2, N_HID], F32)
+        t = {}
+
+        def dm():
+            if "dm" not in t:
+                t["dm"] = mx.tile([P, 512], F32, tag="mx", name="dmb")
+            nc.tensor.matmul(out=t["dm"][:], lhsT=ones_bf[:], rhs=dz[:], start=True, stop=True)
+
+        def bc():
+            nc.vector.tensor_copy(out=zt[:], in_=zt_bf[:])
+
+        def bt():
+            t["bt"] = mx.tile([P, 512], F32, tag="mx", name="bt")
+            nc.tensor.transpose(t["bt"][:, 0:P], zt[:], ident[:])
+            t["bb"] = mx.tile([P, 512], F32, tag="mx", name="bb")
+            nc.tensor.matmul(out=t["bb"][:, 0:N_HID], lhsT=ones_bf[:], rhs=zb_bf[:], start=True, stop=True)
+
+        def bv():
+            nc.vector.tensor_copy(out=bias_sb[:], in_=t["bt"][:, 0:8])
+            nc.vector.tensor_tensor(out=bf_sum[:], in0=bias_sb[:, 4:6], in1=bias_sb[:, 6:8], op=ALU.add)
+            nc.vector.tensor_scalar_mul(out=bf_half[:], in0=bf_sum[:], scalar1=0.5)
+
+        def bw(eng):
+            for r in range(2):
+                copy_on(eng, bp_bc[:, r, :], t["bb"][:, 0:N_HID])
+
+        wc = [const.tile([P, 2, 2, P], U32, name="wc%d" % w, align_bytes=64) for w in range(4)]
+        ws = [const.tile([P, 2, 2, P], U8, name="ws%d" % w, align_bytes=64) for w in range(4)]
+        wc.append(const.tile([P, 2, N_HID], U32, name="wc4", align_bytes=64))
+        ws.append(const.tile([P, 2, N_HID], U8, name="ws4", align_bytes=64))
+
+        def copy_on(eng, out, in_):
+            if eng == "S":
+                nc.scalar.copy(out=out, in_=in_)
+            else:
+                nc.vector.tensor_copy(out=out, in_=in_)
+
+        def mm(w, hf):
+            nc.vector.tensor_tensor(out=w_sb[w][hf][:], in0=w_sb[w][hf][:], in1=mask_sb[hf][:], op=ALU.mult)
+
+        def wt(w, hf):
+            bank = tr.tile([P, 512], F32, tag="tr", name="wt")
+            t["wt", w, hf] = bank
+            ww = w_sb[w][hf][:].bitcast(F32)
+            for b in range(4):
+                nc.tensor.transpose(bank[:, P * b : P * (b + 1)], ww[:, 256 * (b // 2) + b % 2 : 256 * (b // 2 + 1) : 2], ident[:])
+
+        def wcp(w, hf, eng):
+            if ("wg", w) not in t:
+                t["wg", w] = wgr.tile([P, 2, 2, P, 2], F32, tag="wg", name="wg", align_bytes=64)
+            if w < 4:
+                dst = t["wg", w][:, hf, :, :, :]
+            else:
+                dst = t["wg", w][:].rearrange("q a b c u -> q a (b c) u")[:, :, P * hf : P * (hf + 1), :]
+            copy_on(eng, dst, t["wt", w, hf][:].rearrange("q (g u c) -> q g c u", g=2, u=2))
+
+        def wq(w):
+            nc.vector.quantize_mx(
+                out=wc[w][:].rearrange("q g c -> q (g c)").bitcast(FP8X4),
+                scales=ws[w][:].rearrange("q g c -> q (g c)"),
+                in_=t["wg", w][:].rearrange("q a b c u -> q (a b c u)").bitcast(BF16),
+            )
+
+        def wh(w, hf):
+            nc.vector.quantize_mx(
+                out=wc[w][:, hf, :, :].rearrange("q g c -> q (g c)").bitcast(FP8X4),
+                scales=ws[w][:, hf, :, :].rearrange("q g c -> q (g c)"),
+                in_=t["wg", w][:, hf, :, :, :].rearrange("q g c u -> q (g c u)").bitcast(BF16),
+            )
+
+        def xt(s, j):
+            bank = tr.tile([P, 512], F32, tag="tr", name="xt")
+            t["xt", s, j] = bank
+            xw = x_sb[s][:, j, :].bitcast(F32)
+            for b in range(4):
+                nc.tensor.transpose(bank[:, P * b : P * (b + 1)], xw[:, 256 * (b // 2) + b % 2 : 256 * (b // 2 + 1) : 2], ident[:])
+
+        def xcp(s, j, eng):
+            if ("xg", s) not in t:
+                t["xg", s] = xgr.tile([P, 2, SB, 2], F32, tag="xg", name="xg", align_bytes=64)
+            copy_on(
+                eng,
+                t["xg", s][:, :, P * j : P * (j + 1), :],
+                t["xt", s, j][:].rearrange("q (g u c) -> q g c u", g=2, u=2),
+            )
+
+        def xqz(s):
+            t["xc", s] = xq.tile([P, 2, SB], U32, tag="xc", name="xc", align_bytes=64)
+            t["xs", s] = xq.tile([P, 2, SB], U8, tag="xs", name="xs", align_bytes=64)
+            nc.vector.quantize_mx(
+                out=t["xc", s][:].rearrange("q g c -> q (g c)").bitcast(FP8X4),
+                scales=t["xs", s][:].rearrange("q g c -> q (g c)"),
+                in_=t["xg", s][:].rearrange("q g c u -> q (g c u)").bitcast(BF16),
+            )
+
+        layers = {"g": [0], "h": [1], "f": [2, 3]}
+
+        def mxl(s, lay, hf):
+            acc = mx.tile([P, 512], F32, tag="mx", name="acc")
+            t["acc", s, lay, hf] = acc
+            wlist = layers[lay]
+            n = 2 * len(wlist)
+            i = 0
+            for w in wlist:
+                for g in range(2):
+                    nc.tensor.matmul_mx(
+                        out=acc[:],
+                        lhsT=wc[w][:, hf, g, :].bitcast(FP8X4),
+                        lhsT_scale=ws[w][:, hf, g, :],
+                        rhs=t["xc", s][:, g, :].bitcast(FP8X4),
+                        rhs_scale=t["xs", s][:, g, :],
+                        start=(i == 0),
+                        stop=(i == n - 1),
+                    )
+                    i += 1
+
+        def actl(s, lay, hf):
+            if (lay, s) not in t:
+                t[lay, s] = act.tile([P, 2, SB], F32, tag=lay, name="a" + lay)
+            if lay == "g":
+                bias, scale = bias_sb[:, hf : hf + 1], 1.0
+            elif lay == "h":
+                bias, scale = bias_sb[:, 2 + hf : 3 + hf], 1.0
+            else:
+                bias, scale = bf_half[:, hf : hf + 1], 0.5
+            nc.scalar.activation(out=t[lay, s][:, hf, :], in_=t["acc", s, lay, hf][:], func=ACT.Tanh, bias=bias, scale=scale)
+
+        def actf2(s, k):
+            hf, c = k // 2, k % 2
+            cols = slice(N_HID * c, N_HID * (c + 1))
+            if ("f", s) not in t:
+                t["f", s] = act.tile([P, 2, SB], F32, tag="f", name="af")
+            nc.scalar.activation(
+                out=t["f", s][:, hf, cols], in_=t["acc", s, "f", hf][:, cols], func=ACT.Tanh, bias=bf_half[:, hf : hf + 1], scale=0.5
+            )
+
+        def ee2(s, k):
+            hf, c = k // 2, k % 2
+            cols = slice(N_HID * c, N_HID * (c + 1))
+            nc.vector.scalar_tensor_tensor(
+                out=t["d", s][:, hf, cols], in0=t["f", s][:, hf, cols], scalar=1.0, in1=t["d", s][:, hf, cols], op0=ALU.add, op1=ALU.mult
+            )
+
+        def nn2(s, k):
+            hf, c = k // 2, k % 2
+            cols = slice(N_HID * c, N_HID * (c + 1))
+            if ("nh", s) not in t:
+                t["nh", s] = ep.tile([P, 2, SB], F32, tag="nh", name="nh")
+            nc.vector.scalar_tensor_tensor(
+                out=t["nh", s][:, hf, cols], in0=t["d", s][:, hf, cols], scalar=0.5, in1=t["g", s][:, hf, cols], op0=ALU.mult, op1=ALU.add
+            )
+
+        def mxp(s, jp):
+            acc = mx.tile([P, 512], F32, tag="mx", name="accp")
+            t["accp", s, jp] = acc
+            for jj in range(2):
+                cols = slice(P * (2 * jp + jj), P * (2 * jp + jj + 1))
+                for g in range(2):
+                    nc.tensor.matmul_mx(
+                        out=acc[:, N_HID * jj : N_HID * (jj + 1)],
+                        lhsT=t["xc", s][:, g, cols].bitcast(FP8X4),
+                        lhsT_scale=t["xs", s][:, g, cols],
+                        rhs=wc[4][:, g, :].bitcast(FP8X4),
+                        rhs_scale=ws[4][:, g, :],
+                        start=(g == 0),
+                        stop=(g == 1),
+                    )
+
+        def half(tile_, jp):
+            return tile_[:, 2 * jp : 2 * jp + 2, :].rearrange("p a f -> p (a f)")
+
+        def pbias(s, jp):
+            if ("pb", s) not in t:
+                t["pb", s] = outp.tile([P, JT, N_HID], F32, tag="pb", name="pb")
+            nc.vector.tensor_tensor(
+                out=half(t["pb", s], jp), in0=t["accp", s, jp][:], in1=bp_bc[:].rearrange("p a f -> p (a f)"), op=ALU.add
+            )
+
+        def dd(s, hf):
+            if ("d", s) not in t:
+                t["d", s] = ep.tile([P, 2, SB], F32, tag="d", name="d")
+            nc.vector.tensor_tensor(out=t["d", s][:, hf, :], in0=t["h", s][:, hf, :], in1=t["g", s][:, hf, :], op=ALU.subtract)
+
+        def ee(s, hf):
+            nc.vector.scalar_tensor_tensor(
+                out=t["d", s][:, hf, :], in0=t["f", s][:, hf, :], scalar=1.0, in1=t["d", s][:, hf, :], op0=ALU.add, op1=ALU.mult
+            )
+
+        def nn(s, hf):
+            if ("nh", s) not in t:
+                t["nh", s] = ep.tile([P, 2, SB], F32, tag="nh", name="nh")
+            nc.vector.scalar_tensor_tensor(
+                out=t["nh", s][:, hf, :], in0=t["d", s][:, hf, :], scalar=0.5, in1=t["g", s][:, hf, :], op0=ALU.mult, op1=ALU.add
+            )
+
+        def nt(s, jp):
+            bank = tr.tile([P, 512], F32, tag="tr", name="nt")
+            t["nt", s, jp] = bank
+            for jj in range(2):
+                j = 2 * jp + jj
+                for hf in range(2):
+                    o = N_HID * jj + P * hf
+                    nc.tensor.transpose(bank[:, o : o + P], t["nh", s][:, hf, P * j : P * (j + 1)], ident[:])
+
+        def ncp(s, jp, eng):
+            if ("nht", s) not in t:
+                t["nht", s] = outp.tile([P, JT, N_HID], F32, tag="nht", name="nht")
+            copy_on(eng, half(t["nht", s], jp), t["nt", s, jp][:])
+
+        def yh(s, jp):
+            if ("y", s) not in t:
+                t["y", s] = outp.tile([P, JT, N_HID], F32, tag="y", name="y")
+            nc.vector.tensor_tensor(out=half(t["y", s], jp), in0=half(t["nht", s], jp), in1=half(t["pb", s], jp), op=ALU.add)
+
+        def yy(s):
+            t["y", s] = outp.tile([P, JT, N_HID], F32, tag="y", name="y")
+            nc.vector.tensor_tensor(out=t["y", s][:], in0=t["nht", s][:], in1=t["pb", s][:], op=ALU.add)
+
+        def store(dst, key, s, jp):
+            view = dst[SB * s : SB * (s + 1), :].rearrange("(p j) f -> p j f", j=JT)
+            if jp is None:
+                nc.sync.dma_start(out=view, in_=t[key, s][:])
+            else:
+                nc.sync.dma_start(out=view[:, 2 * jp : 2 * jp + 2, :], in_=t[key, s][:, 2 * jp : 2 * jp + 2, :])
+
+        dm()
+        mm(0, 0)
+        dm()
+        dm()
+        dm()
+        dm()
+        dm()
+        dm()
+        dm()
+        xt(0, 1)
+        xt(0, 3)
+        mm(0, 1)
+        xcp(0, 1, "S")
+        mm(1, 0)
+        xt(0, 2)
+        xt(0, 0)
+        xcp(0, 2, "S")
+        dm()
+        dm()
+        xcp(0, 0, "S")
+        xcp(0, 3, "S")
+        wt(0, 1)
+        wcp(0, 1, "S")
+        xqz(0)
+        dm()
+        dm()
+        wt(1, 0)
+        wt(0, 0)
+        wh(0, 1)
+        mxl(0, "g", 1)
+        mm(1, 1)
+        wcp(1, 0, "S")
+        wt(1, 1)
+        wcp(0, 0, "S")
+        wh(1, 0)
+        wcp(1, 1, "S")
+        bc()
+        xt(1, 2)
+        bt()
+        xt(1, 3)
+        wh(0, 0)
+        xcp(1, 2, "S")
+        mm(2, 0)
+        bv()
+        xcp(1, 3, "V")
+        mxl(0, "g", 0)
+        wh(1, 1)
+        actl(0, "g", 1)
+        xt(1, 1)
+        xt(1, 0)
+        mm(2, 1)
+        bw("S")
+        mxl(0, "h", 1)
+        mxl(0, "h", 0)
+        xcp(1, 0, "S")
+        mm(3, 1)
+        wt(2, 0)
+        wt(3, 1)
+        mm(3, 0)
+        xcp(1, 1, "S")
+        wt(3, 0)
+        actl(0, "g", 0)
+        actl(0, "h", 0)
+        xqz(1)
+        actl(0, "h", 1)
+        wt(2, 1)
+        wcp(3, 0, "V")
+        wcp(3, 1, "V")
+        wh(3, 0)
+        mxl(1, "g", 0)
+        mxl(1, "h", 1)
+        wcp(2, 0, "S")
+        mxl(1, "g", 1)
+        actl(1, "g", 0)
+        wh(3, 1)
+        wh(2, 0)
+        mxl(1, "h", 0)
+        dd(0, 0)
+        wcp(2, 1, "S")
+        wh(2, 1)
+        actl(1, "h", 1)
+        mm(4, 1)
+        mm(4, 0)
+        actl(1, "g", 1)
+        actl(1, "h", 0)
+        dd(1, 0)
+        mxl(0, "f", 0)
+        actl(0, "f", 0)
+        ee(0, 0)
+        dd(0, 1)
+        nn(0, 0)
+        mxl(0, "f", 1)
+        wt(4, 0)
+        wt(4, 1)
+        xt(2, 0)
+        xt(2, 1)
+        mxl(1, "f", 0)
+        wcp(4, 0, "S")
+        actl(0, "f", 1)
+        wcp(4, 1, "S")
+        mxl(1, "f", 1)
+        xcp(2, 1, "S")
+        xcp(2, 0, "S")
+        xt(2, 3)
+        xt(2, 2)
+        actl(1, "f", 0)
+        ee(0, 1)
+        dd(1, 1)
+        nn(0, 1)
+        nt(0, 1)
+        wq(4)
+        nt(0, 0)
+        mxp(0, 0)
+        ee(1, 0)
+        actl(1, "f", 1)
+        mxp(1, 0)
+        ee(1, 1)
+        nn(1, 0)
+        ncp(0, 0, "S")
+        ncp(0, 1, "S")
+        pbias(0, 0)
+        mxp(1, 1)
+        xcp(2, 2, "S")
+        mxp(0, 1)
+        nn(1, 1)
+        xcp(2, 3, "S")
+        pbias(1, 0)
+        xt(3, 1)
+        xt(3, 0)
+        xqz(2)
+        xt(3, 2)
+        xt(3, 3)
+        pbias(0, 1)
+        pbias(1, 1)
+        yy(0)
+        xcp(3, 0, "S")
+        xcp(3, 3, "S")
+        store(out_1, "nht", 0, None)
+        store(out_0, "y", 0, None)
+        xcp(3, 1, "S")
+        xcp(3, 2, "S")
+        mxl(2, "g", 0)
+        mxl(2, "h", 0)
+        mxl(2, "f", 0)
+        actl(2, "g", 0)
+        nt(1, 0)
+        nt(1, 1)
+        xt(4, 0)
+        xqz(3)
+        actl(2, "h", 0)
+        dd(2, 0)
+        actl(2, "f", 0)
+        mxl(2, "g", 1)
+        mxl(2, "h", 1)
+        ee(2, 0)
+        ncp(1, 0, "S")
+        mxl(2, "f", 1)
+        mxp(2, 0)
+        ncp(1, 1, "S")
+        nn(2, 0)
+        xcp(4, 0, "S")
+        actl(2, "g", 1)
+        yy(1)
+        actl(2, "h", 1)
+        store(out_1, "nht", 1, None)
+        store(out_0, "y", 1, None)
+        mxp(2, 1)
+        dd(2, 1)
+        xt(4, 1)
+        actl(2, "f", 1)
+        xcp(4, 1, "S")
+        xt(4, 2)
+        pbias(2, 0)
+        ee(2, 1)
+        xt(4, 3)
+        pbias(2, 1)
+        xcp(4, 2, "S")
+        nn(2, 1)
+        xcp(4, 3, "S")
+        mxl(3, "g", 0)
+        mxl(3, "h", 0)
+        mxl(3, "f", 0)
+        actl(3, "g", 0)
+        nt(2, 0)
+        nt(2, 1)
+        xt(5, 0)
+        xqz(4)
+        actl(3, "h", 0)
+        dd(3, 0)
+        actl(3, "f", 0)
+        mxl(3, "g", 1)
+        mxl(3, "h", 1)
+        ee(3, 0)
+        ncp(2, 0, "S")
+        mxl(3, "f", 1)
+        mxp(3, 0)
+        ncp(2, 1, "S")
+        nn(3, 0)
+        xcp(5, 0, "S")
+        actl(3, "g", 1)
+        yy(2)
+        actl(3, "h", 1)
+        store(out_1, "nht", 2, None)
+        store(out_0, "y", 2, None)
+        mxp(3, 1)
+        dd(3, 1)
+        xt(5, 1)
+        actl(3, "f", 1)
+        xcp(5, 1, "S")
+        xt(5, 2)
+        pbias(3, 0)
+        ee(3, 1)
+        xt(5, 3)
+        pbias(3, 1)
+        xcp(5, 2, "S")
+        nn(3, 1)
+        xcp(5, 3, "S")
+        mxl(4, "g", 0)
+        mxl(4, "h", 0)
+        mxl(4, "f", 0)
+        actl(4, "g", 0)
+        nt(3, 0)
+        nt(3, 1)
+        xt(6, 0)
+        xqz(5)
+        actl(4, "h", 0)
+        dd(4, 0)
+        actl(4, "f", 0)
+        mxl(4, "g", 1)
+        mxl(4, "h", 1)
+        ee(4, 0)
+        ncp(3, 0, "S")
+        mxl(4, "f", 1)
+        mxp(4, 0)
+        ncp(3, 1, "S")
+        nn(4, 0)
+        xcp(6, 0, "S")
+        actl(4, "g", 1)
+        yy(3)
+        actl(4, "h", 1)
+        store(out_1, "nht", 3, None)
+        store(out_0, "y", 3, None)
+        mxp(4, 1)
+        dd(4, 1)
+        xt(6, 1)
+        actl(4, "f", 1)
+        xcp(6, 1, "S")
+        xt(6, 2)
+        pbias(4, 0)
+        ee(4, 1)
+        xt(6, 3)
+        pbias(4, 1)
+        xcp(6, 2, "S")
+        nn(4, 1)
+        xcp(6, 3, "S")
+        mxl(5, "g", 0)
+        mxl(5, "h", 0)
+        mxl(5, "f", 0)
+        actl(5, "g", 0)
+        nt(4, 0)
+        nt(4, 1)
+        xt(7, 0)
+        xqz(6)
+        actl(5, "h", 0)
+        dd(5, 0)
+        actl(5, "f", 0)
+        mxl(5, "g", 1)
+        mxl(5, "h", 1)
+        ee(5, 0)
+        ncp(4, 0, "S")
+        mxl(5, "f", 1)
+        mxp(5, 0)
+        ncp(4, 1, "S")
+        nn(5, 0)
+        xcp(7, 0, "S")
+        actl(5, "g", 1)
+        yy(4)
+        actl(5, "h", 1)
+        store(out_1, "nht", 4, None)
+        store(out_0, "y", 4, None)
+        mxp(5, 1)
+        dd(5, 1)
+        xt(7, 1)
+        actl(5, "f", 1)
+        xcp(7, 1, "S")
+        xt(7, 2)
+        pbias(5, 0)
+        ee(5, 1)
+        xt(7, 3)
+        pbias(5, 1)
+        xcp(7, 2, "S")
+        nn(5, 1)
+        xcp(7, 3, "S")
+        mxl(6, "g", 0)
+        mxl(6, "h", 0)
+        mxl(6, "f", 0)
+        actl(6, "g", 0)
+        nt(5, 0)
+        nt(5, 1)
+        xqz(7)
+        actl(6, "h", 0)
+        dd(6, 0)
+        actl(6, "f", 0)
+        mxl(6, "g", 1)
+        mxl(6, "h", 1)
+        ee(6, 0)
+        ncp(5, 0, "S")
+        mxl(6, "f", 1)
+        mxp(6, 0)
+        ncp(5, 1, "S")
+        nn(6, 0)
+        actl(6, "g", 1)
+        yy(5)
+        actl(6, "h", 1)
+        store(out_1, "nht", 5, None)
+        store(out_0, "y", 5, None)
+        mxp(6, 1)
+        dd(6, 1)
+        actl(6, "f", 1)
+        pbias(6, 0)
+        ee(6, 1)
+        pbias(6, 1)
+        nn(6, 1)
+        mxl(7, "h", 0)
+        mxl(7, "g", 0)
+        mxl(7, "f", 0)
+        actl(7, "h", 0)
+        nt(6, 0)
+        nt(6, 1)
+        mxl(7, "g", 1)
+        actl(7, "g", 0)
+        actl(7, "f", 0)
+        ncp(6, 1, "S")
+        dd(7, 0)
+        mxl(7, "h", 1)
+        actl(7, "g", 1)
+        ncp(6, 0, "V")
+        mxl(7, "f", 1)
+        actl(7, "h", 1)
+        ee(7, 0)
+        yy(6)
+        actf2(7, 2)
+        dd(7, 1)
+        nn(7, 0)
+        mxp(7, 0)
+        actf2(7, 3)
+        ee2(7, 2)
+        ee2(7, 3)
+        mxp(7, 1)
+        nn2(7, 2)
+        nt(7, 0)
+        nn2(7, 3)
+        store(out_1, "nht", 6, None)
+        store(out_0, "y", 6, None)
+        pbias(7, 0)
+        nt(7, 1)
+        ncp(7, 0, "S")
+        ncp(7, 1, "S")
+        pbias(7, 1)
+        yh(7, 0)
+        store(out_1, "nht", 7, 0)
+        store(out_1, "nht", 7, 1)
+        store(out_0, "y", 7, 0)
+        yh(7, 1)
+        store(out_0, "y", 7, 1)

@@ -29,7 +29,8 @@ def tile_ncpliquidcell_t_kernel(
         const = ctx.enter_context(tc.tile_pool(name="const", bufs=1))
         wraw = ctx.enter_context(tc.tile_pool(name="wraw", bufs=10))
         wgr = ctx.enter_context(tc.tile_pool(name="wgr", bufs=2))
-        xin = ctx.enter_context(tc.tile_pool(name="xin", bufs=NSB))
+        xin = ctx.enter_context(tc.tile_pool(name="xin", bufs=NSB - 1))
+        xre = ctx.enter_context(tc.tile_pool(name="xre", bufs=4))
         xgr = ctx.enter_context(tc.tile_pool(name="xgr", bufs=2))
         xq = ctx.enter_context(tc.tile_pool(name="xq", bufs=3))
         act = ctx.enter_context(tc.tile_pool(name="act", bufs=3))
@@ -59,7 +60,7 @@ def tile_ncpliquidcell_t_kernel(
 
         mask_sb = [const.tile([P, K], BF16, name="mask%d" % hf) for hf in range(2)]
         w_sb = [[wraw.tile([P, K], BF16, name="w%d_%d" % (w, hf), tag="w") for hf in range(2)] for w in range(5)]
-        x_sb = [xin.tile([P, JT, K], BF16, name="x%d" % s, tag="x") for s in range(NSB)]
+        x_sb = {}
 
         def load_m(hf):
             nc.sync.dma_start(out=mask_sb[hf][:], in_=mask[P * hf : P * (hf + 1), :])
@@ -69,6 +70,7 @@ def tile_ncpliquidcell_t_kernel(
 
         def load_x(s):
             rows = slice(SB * s, SB * (s + 1))
+            x_sb[s] = xin.tile([P, JT, K], BF16, name="x", tag="x")
             nc.sync.dma_start(out=x_sb[s][:, :, 0:IN_F], in_=x[rows, :].rearrange("(p j) k -> p j k", j=JT))
             nc.sync.dma_start(out=x_sb[s][:, :, IN_F:K], in_=hidden[rows, :].rearrange("(p j) k -> p j k", j=JT))
 
@@ -91,7 +93,6 @@ def tile_ncpliquidcell_t_kernel(
         load_x(4)
         load_x(5)
         load_x(6)
-        load_x(7)
 
         zt = const.tile([P, P], F32)
         bias_sb = const.tile([P, 8], F32)
@@ -167,12 +168,20 @@ def tile_ncpliquidcell_t_kernel(
                 in_=t["wg", w][:, hf, :, :, :].rearrange("q g c u -> q (g c u)").bitcast(BF16),
             )
 
+        def xr(s, j, eng):
+            t["xr", s, j] = xre.tile([P, 2, 2, P], F32, tag="xr", name="xr")
+            copy_on(eng, t["xr", s, j][:], x_sb[s][:, j, :].bitcast(F32).rearrange("q (g c u) -> q g u c", g=2, u=2))
+
         def xt(s, j):
             bank = tr.tile([P, 512], F32, tag="tr", name="xt")
             t["xt", s, j] = bank
             xw = x_sb[s][:, j, :].bitcast(F32)
             for b in range(4):
-                nc.tensor.transpose(bank[:, P * b : P * (b + 1)], xw[:, 256 * (b // 2) + b % 2 : 256 * (b // 2 + 1) : 2], ident[:])
+                if ("xr", s, j) in t:
+                    words = t["xr", s, j][:, b // 2, b % 2, :]
+                else:
+                    words = xw[:, 256 * (b // 2) + b % 2 : 256 * (b // 2 + 1) : 2]
+                nc.tensor.transpose(bank[:, P * b : P * (b + 1)], words, ident[:])
 
         def xcp(s, j, eng):
             if ("xg", s) not in t:
@@ -409,6 +418,7 @@ def tile_ncpliquidcell_t_kernel(
         actl(1, "h", 0)
         dd(1, 0)
         mxl(0, "f", 0)
+        load_x(7)
         actl(0, "f", 0)
         ee(0, 0)
         dd(0, 1)
@@ -463,158 +473,53 @@ def tile_ncpliquidcell_t_kernel(
         store(out_0, "y", 0, None)
         xcp(3, 1, "S")
         xcp(3, 2, "S")
-        mxl(2, "g", 0)
-        mxl(2, "h", 0)
-        mxl(2, "f", 0)
-        actl(2, "g", 0)
-        nt(1, 0)
-        nt(1, 1)
-        xt(4, 0)
-        xqz(3)
-        actl(2, "h", 0)
-        dd(2, 0)
-        actl(2, "f", 0)
-        mxl(2, "g", 1)
-        mxl(2, "h", 1)
-        ee(2, 0)
-        ncp(1, 0, "S")
-        mxl(2, "f", 1)
-        mxp(2, 0)
-        ncp(1, 1, "S")
-        nn(2, 0)
-        xcp(4, 0, "S")
-        actl(2, "g", 1)
-        yy(1)
-        actl(2, "h", 1)
-        store(out_1, "nht", 1, None)
-        store(out_0, "y", 1, None)
-        mxp(2, 1)
-        dd(2, 1)
-        xt(4, 1)
-        actl(2, "f", 1)
-        xcp(4, 1, "S")
-        xt(4, 2)
-        pbias(2, 0)
-        ee(2, 1)
-        xt(4, 3)
-        pbias(2, 1)
-        xcp(4, 2, "S")
-        nn(2, 1)
-        xcp(4, 3, "S")
-        mxl(3, "g", 0)
-        mxl(3, "h", 0)
-        mxl(3, "f", 0)
-        actl(3, "g", 0)
-        nt(2, 0)
-        nt(2, 1)
-        xt(5, 0)
-        xqz(4)
-        actl(3, "h", 0)
-        dd(3, 0)
-        actl(3, "f", 0)
-        mxl(3, "g", 1)
-        mxl(3, "h", 1)
-        ee(3, 0)
-        ncp(2, 0, "S")
-        mxl(3, "f", 1)
-        mxp(3, 0)
-        ncp(2, 1, "S")
-        nn(3, 0)
-        xcp(5, 0, "S")
-        actl(3, "g", 1)
-        yy(2)
-        actl(3, "h", 1)
-        store(out_1, "nht", 2, None)
-        store(out_0, "y", 2, None)
-        mxp(3, 1)
-        dd(3, 1)
-        xt(5, 1)
-        actl(3, "f", 1)
-        xcp(5, 1, "S")
-        xt(5, 2)
-        pbias(3, 0)
-        ee(3, 1)
-        xt(5, 3)
-        pbias(3, 1)
-        xcp(5, 2, "S")
-        nn(3, 1)
-        xcp(5, 3, "S")
-        mxl(4, "g", 0)
-        mxl(4, "h", 0)
-        mxl(4, "f", 0)
-        actl(4, "g", 0)
-        nt(3, 0)
-        nt(3, 1)
-        xt(6, 0)
-        xqz(5)
-        actl(4, "h", 0)
-        dd(4, 0)
-        actl(4, "f", 0)
-        mxl(4, "g", 1)
-        mxl(4, "h", 1)
-        ee(4, 0)
-        ncp(3, 0, "S")
-        mxl(4, "f", 1)
-        mxp(4, 0)
-        ncp(3, 1, "S")
-        nn(4, 0)
-        xcp(6, 0, "S")
-        actl(4, "g", 1)
-        yy(3)
-        actl(4, "h", 1)
-        store(out_1, "nht", 3, None)
-        store(out_0, "y", 3, None)
-        mxp(4, 1)
-        dd(4, 1)
-        xt(6, 1)
-        actl(4, "f", 1)
-        xcp(6, 1, "S")
-        xt(6, 2)
-        pbias(4, 0)
-        ee(4, 1)
-        xt(6, 3)
-        pbias(4, 1)
-        xcp(6, 2, "S")
-        nn(4, 1)
-        xcp(6, 3, "S")
-        mxl(5, "g", 0)
-        mxl(5, "h", 0)
-        mxl(5, "f", 0)
-        actl(5, "g", 0)
-        nt(4, 0)
-        nt(4, 1)
-        xt(7, 0)
-        xqz(6)
-        actl(5, "h", 0)
-        dd(5, 0)
-        actl(5, "f", 0)
-        mxl(5, "g", 1)
-        mxl(5, "h", 1)
-        ee(5, 0)
-        ncp(4, 0, "S")
-        mxl(5, "f", 1)
-        mxp(5, 0)
-        ncp(4, 1, "S")
-        nn(5, 0)
-        xcp(7, 0, "S")
-        actl(5, "g", 1)
-        yy(4)
-        actl(5, "h", 1)
-        store(out_1, "nht", 4, None)
-        store(out_0, "y", 4, None)
-        mxp(5, 1)
-        dd(5, 1)
-        xt(7, 1)
-        actl(5, "f", 1)
-        xcp(7, 1, "S")
-        xt(7, 2)
-        pbias(5, 0)
-        ee(5, 1)
-        xt(7, 3)
-        pbias(5, 1)
-        xcp(7, 2, "S")
-        nn(5, 1)
-        xcp(7, 3, "S")
+        for s in range(2, 6):
+            mxl(s, "g", 0)
+            mxl(s, "h", 0)
+            mxl(s, "f", 0)
+            actl(s, "g", 0)
+            nt(s - 1, 0)
+            nt(s - 1, 1)
+            xt(s + 2, 0)
+            if s < 6:
+                xr(s + 2, 1, "V")
+            xqz(s + 1)
+            actl(s, "h", 0)
+            dd(s, 0)
+            if s < 6:
+                xr(s + 2, 3, "S")
+            actl(s, "f", 0)
+            mxl(s, "g", 1)
+            mxl(s, "h", 1)
+            if s < 6:
+                xr(s + 2, 2, "V")
+            ee(s, 0)
+            ncp(s - 1, 0, "S")
+            mxl(s, "f", 1)
+            mxp(s, 0)
+            ncp(s - 1, 1, "S")
+            nn(s, 0)
+            xcp(s + 2, 0, "S")
+            actl(s, "g", 1)
+            yy(s - 1)
+            actl(s, "h", 1)
+            store(out_1, "nht", s - 1, None)
+            store(out_0, "y", s - 1, None)
+            mxp(s, 1)
+            dd(s, 1)
+            xt(s + 2, 1)
+            if s < 5:
+                xr(s + 3, 0, "S")
+            actl(s, "f", 1)
+            xcp(s + 2, 1, "S")
+            xt(s + 2, 2)
+            pbias(s, 0)
+            ee(s, 1)
+            xt(s + 2, 3)
+            pbias(s, 1)
+            xcp(s + 2, 2, "S")
+            nn(s, 1)
+            xcp(s + 2, 3, "S")
         mxl(6, "g", 0)
         mxl(6, "h", 0)
         mxl(6, "f", 0)

@@ -29,8 +29,8 @@ def tile_ncpliquidcell_t_kernel(
         const = ctx.enter_context(tc.tile_pool(name="const", bufs=1))
         wraw = ctx.enter_context(tc.tile_pool(name="wraw", bufs=10))
         wgr = ctx.enter_context(tc.tile_pool(name="wgr", bufs=2))
-        xin = ctx.enter_context(tc.tile_pool(name="xin", bufs=NSB - 1))
-        xre = ctx.enter_context(tc.tile_pool(name="xre", bufs=4))
+        xin = ctx.enter_context(tc.tile_pool(name="xin", bufs=NSB - 2))
+        xre = ctx.enter_context(tc.tile_pool(name="xre", bufs=6))
         xgr = ctx.enter_context(tc.tile_pool(name="xgr", bufs=2))
         xq = ctx.enter_context(tc.tile_pool(name="xq", bufs=3))
         act = ctx.enter_context(tc.tile_pool(name="act", bufs=3))
@@ -74,25 +74,14 @@ def tile_ncpliquidcell_t_kernel(
             nc.sync.dma_start(out=x_sb[s][:, :, 0:IN_F], in_=x[rows, :].rearrange("(p j) k -> p j k", j=JT))
             nc.sync.dma_start(out=x_sb[s][:, :, IN_F:K], in_=hidden[rows, :].rearrange("(p j) k -> p j k", j=JT))
 
-        load_x(0)
-        load_m(0)
-        load_w(0, 0)
-        load_m(1)
-        load_w(0, 1)
-        load_w(1, 0)
-        load_w(1, 1)
-        load_x(1)
-        load_w(2, 0)
-        load_w(2, 1)
-        load_w(3, 0)
-        load_w(3, 1)
-        load_w(4, 0)
-        load_w(4, 1)
-        load_x(2)
-        load_x(3)
-        load_x(4)
-        load_x(5)
-        load_x(6)
+
+        def load_xh(s, h):
+            js = slice(2 * h, 2 * h + 2)
+            if s not in x_sb:
+                x_sb[s] = xin.tile([P, JT, K], BF16, name="x", tag="x")
+            for src, cols in ((x, slice(0, IN_F)), (hidden, slice(IN_F, K))):
+                view = src[SB * s : SB * (s + 1), :].rearrange("(p j) k -> p j k", j=JT)
+                nc.sync.dma_start(out=x_sb[s][:, js, cols], in_=view[:, js, :])
 
         zt = const.tile([P, P], F32)
         bias_sb = const.tile([P, 8], F32)
@@ -112,8 +101,7 @@ def tile_ncpliquidcell_t_kernel(
         def bt():
             t["bt"] = mx.tile([P, 512], F32, tag="mx", name="bt")
             nc.tensor.transpose(t["bt"][:, 0:P], zt[:], ident[:])
-            t["bb"] = mx.tile([P, 512], F32, tag="mx", name="bb")
-            nc.tensor.matmul(out=t["bb"][:, 0:N_HID], lhsT=ones_bf[:], rhs=zb_bf[:], start=True, stop=True)
+            nc.tensor.matmul(out=t["bt"][:, P : P + N_HID], lhsT=ones_bf[:], rhs=zb_bf[:], start=True, stop=True)
 
         def bv():
             nc.vector.tensor_copy(out=bias_sb[:], in_=t["bt"][:, 0:8])
@@ -122,7 +110,7 @@ def tile_ncpliquidcell_t_kernel(
 
         def bw(eng):
             for r in range(2):
-                copy_on(eng, bp_bc[:, r, :], t["bb"][:, 0:N_HID])
+                copy_on(eng, bp_bc[:, r, :], t["bt"][:, P : P + N_HID])
 
         wc = [const.tile([P, 2, 2, P], U32, name="wc%d" % w, align_bytes=64) for w in range(4)]
         ws = [const.tile([P, 2, 2, P], U8, name="ws%d" % w, align_bytes=64) for w in range(4)]
@@ -143,7 +131,7 @@ def tile_ncpliquidcell_t_kernel(
             t["wt", w, hf] = bank
             ww = w_sb[w][hf][:].bitcast(F32)
             for b in range(4):
-                nc.tensor.transpose(bank[:, P * b : P * (b + 1)], ww[:, 256 * (b // 2) + b % 2 : 256 * (b // 2 + 1) : 2], ident[:])
+                nc.tensor.transpose(bank[:, P * b : P * (b + 1)], ww[:, 2 * P * (b // 2) + b % 2 : 2 * P * (b // 2 + 1) : 2], ident[:])
 
         def wcp(w, hf, eng):
             if ("wg", w) not in t:
@@ -301,6 +289,21 @@ def tile_ncpliquidcell_t_kernel(
                 out=t["nh", s][:, hf, :], in0=t["d", s][:, hf, :], scalar=0.5, in1=t["g", s][:, hf, :], op0=ALU.mult, op1=ALU.add
             )
 
+        def ddm(s):
+            t["d", s] = ep.tile([P, 2, SB], F32, tag="d", name="d")
+            nc.vector.tensor_tensor(out=t["d", s][:], in0=t["h", s][:], in1=t["g", s][:], op=ALU.subtract)
+
+        def eem(s):
+            nc.vector.scalar_tensor_tensor(
+                out=t["d", s][:], in0=t["f", s][:], scalar=1.0, in1=t["d", s][:], op0=ALU.add, op1=ALU.mult
+            )
+
+        def nnm(s):
+            t["nh", s] = ep.tile([P, 2, SB], F32, tag="nh", name="nh")
+            nc.vector.scalar_tensor_tensor(
+                out=t["nh", s][:], in0=t["d", s][:], scalar=0.5, in1=t["g", s][:], op0=ALU.mult, op1=ALU.add
+            )
+
         def nt(s, jp):
             bank = tr.tile([P, 512], F32, tag="tr", name="nt")
             t["nt", s, jp] = bank
@@ -331,8 +334,8 @@ def tile_ncpliquidcell_t_kernel(
             else:
                 nc.sync.dma_start(out=view[:, 2 * jp : 2 * jp + 2, :], in_=t[key, s][:, 2 * jp : 2 * jp + 2, :])
 
+        load_x(0)
         dm()
-        mm(0, 0)
         dm()
         dm()
         dm()
@@ -341,254 +344,398 @@ def tile_ncpliquidcell_t_kernel(
         dm()
         dm()
         xt(0, 1)
-        xt(0, 3)
-        mm(0, 1)
         xcp(0, 1, "S")
-        mm(1, 0)
+        load_m(0)
+        xt(0, 3)
         xt(0, 2)
-        xt(0, 0)
         xcp(0, 2, "S")
-        dm()
-        dm()
+        load_w(0, 0)
+        mm(0, 0)
+        xt(0, 0)
         xcp(0, 0, "S")
         xcp(0, 3, "S")
+        dm()
+        load_m(1)
+        dm()
+        load_w(0, 1)
+        mm(0, 1)
         wt(0, 1)
         wcp(0, 1, "S")
+        dm()
+        dm()
+        load_w(1, 0)
+        mm(1, 0)
         xqz(0)
-        dm()
-        dm()
-        wt(1, 0)
-        wt(0, 0)
         wh(0, 1)
-        mxl(0, "g", 1)
-        mm(1, 1)
+        wt(1, 0)
         wcp(1, 0, "S")
-        wt(1, 1)
+        wt(0, 0)
         wcp(0, 0, "S")
+        load_w(1, 1)
+        mm(1, 1)
         wh(1, 0)
-        wcp(1, 1, "S")
         bc()
+        wh(0, 0)
+        mxl(0, "g", 1)
+        load_x(1)
+        wt(1, 1)
+        wcp(1, 1, "S")
         xt(1, 2)
+        xcp(1, 2, "S")
         bt()
         xt(1, 3)
-        wh(0, 0)
-        xcp(1, 2, "S")
+        mxl(0, "g", 0)
+        load_w(2, 0)
         mm(2, 0)
         bv()
-        xcp(1, 3, "V")
-        mxl(0, "g", 0)
-        wh(1, 1)
         actl(0, "g", 1)
+        bw("S")
+        xcp(1, 3, "V")
+        wh(1, 1)
         xt(1, 1)
         xt(1, 0)
-        mm(2, 1)
-        bw("S")
-        mxl(0, "h", 1)
-        mxl(0, "h", 0)
         xcp(1, 0, "S")
-        mm(3, 1)
-        wt(2, 0)
-        wt(3, 1)
-        mm(3, 0)
         xcp(1, 1, "S")
-        wt(3, 0)
         actl(0, "g", 0)
+        load_w(2, 1)
+        mm(2, 1)
+        mxl(0, "h", 1)
+        load_w(3, 0)
+        mxl(0, "h", 0)
         actl(0, "h", 0)
-        xqz(1)
         actl(0, "h", 1)
-        wt(2, 1)
+        load_w(3, 1)
+        mm(3, 1)
+        mm(3, 0)
+        xqz(1)
+        wt(2, 0)
+        wcp(2, 0, "S")
+        wt(3, 1)
+        load_w(4, 0)
+        wt(3, 0)
         wcp(3, 0, "V")
         wcp(3, 1, "V")
+        load_w(4, 1)
+        wt(2, 1)
         wh(3, 0)
         mxl(1, "g", 0)
-        mxl(1, "h", 1)
-        wcp(2, 0, "S")
-        mxl(1, "g", 1)
         actl(1, "g", 0)
-        wh(3, 1)
-        wh(2, 0)
-        mxl(1, "h", 0)
-        dd(0, 0)
         wcp(2, 1, "S")
-        wh(2, 1)
+        wh(3, 1)
+        load_x(2)
+        wh(2, 0)
+        mxl(1, "h", 1)
         actl(1, "h", 1)
-        mm(4, 1)
-        mm(4, 0)
+        dd(0, 0)
+        mxl(1, "g", 1)
         actl(1, "g", 1)
+        wh(2, 1)
+        mm(4, 1)
+        mxl(1, "h", 0)
         actl(1, "h", 0)
-        dd(1, 0)
+        mm(4, 0)
         mxl(0, "f", 0)
-        load_x(7)
         actl(0, "f", 0)
-        ee(0, 0)
-        dd(0, 1)
-        nn(0, 0)
+        xr(2, 3, "S")
+        load_x(3)
+        dd(1, 0)
         mxl(0, "f", 1)
+        ee(0, 0)
         wt(4, 0)
-        wt(4, 1)
-        xt(2, 0)
-        xt(2, 1)
-        mxl(1, "f", 0)
         wcp(4, 0, "S")
         actl(0, "f", 1)
+        dd(0, 1)
+        wt(4, 1)
         wcp(4, 1, "S")
-        mxl(1, "f", 1)
+        xt(2, 0)
+        nn(0, 0)
+        xt(2, 1)
         xcp(2, 1, "S")
         xcp(2, 0, "S")
-        xt(2, 3)
-        xt(2, 2)
-        actl(1, "f", 0)
+        load_x(4)
+        mxl(1, "f", 0)
         ee(0, 1)
+        actl(1, "f", 0)
+        mxl(1, "f", 1)
         dd(1, 1)
-        nn(0, 1)
-        nt(0, 1)
-        wq(4)
-        nt(0, 0)
-        mxp(0, 0)
-        ee(1, 0)
         actl(1, "f", 1)
-        mxp(1, 0)
-        ee(1, 1)
-        nn(1, 0)
+        xt(2, 3)
+        nn(0, 1)
+        xr(3, 1, "S")
+        xt(2, 2)
+        xr(3, 0, "S")
+        wq(4)
+        nt(0, 1)
+        nt(0, 0)
         ncp(0, 0, "S")
+        load_x(5)
+        ee(1, 0)
+        mxp(0, 0)
         ncp(0, 1, "S")
-        pbias(0, 0)
-        mxp(1, 1)
+        ee(1, 1)
+        mxp(1, 0)
         xcp(2, 2, "S")
-        mxp(0, 1)
-        nn(1, 1)
+        mxp(1, 1)
+        nn(1, 0)
         xcp(2, 3, "S")
-        pbias(1, 0)
+        mxp(0, 1)
+        xr(3, 2, "V")
+        xr(4, 0, "S")
+        xr(3, 3, "V")
+        load_x(6)
         xt(3, 1)
+        xr(4, 3, "S")
+        pbias(0, 0)
         xt(3, 0)
-        xqz(2)
-        xt(3, 2)
-        xt(3, 3)
-        pbias(0, 1)
-        pbias(1, 1)
-        yy(0)
         xcp(3, 0, "S")
+        xt(3, 2)
+        nn(1, 1)
+        xt(3, 3)
         xcp(3, 3, "S")
-        store(out_1, "nht", 0, None)
-        store(out_0, "y", 0, None)
+        pbias(1, 0)
         xcp(3, 1, "S")
+        xqz(2)
+        mxl(2, "g", 0)
+        mxl(2, "h", 0)
         xcp(3, 2, "S")
-        for s in range(2, 6):
-            mxl(s, "g", 0)
-            mxl(s, "h", 0)
-            mxl(s, "f", 0)
-            actl(s, "g", 0)
-            nt(s - 1, 0)
-            nt(s - 1, 1)
-            xt(s + 2, 0)
-            if s < 6:
-                xr(s + 2, 1, "V")
-            xqz(s + 1)
-            actl(s, "h", 0)
-            dd(s, 0)
-            if s < 6:
-                xr(s + 2, 3, "S")
-            actl(s, "f", 0)
-            mxl(s, "g", 1)
-            mxl(s, "h", 1)
-            if s < 6:
-                xr(s + 2, 2, "V")
-            ee(s, 0)
-            ncp(s - 1, 0, "S")
-            mxl(s, "f", 1)
-            mxp(s, 0)
-            ncp(s - 1, 1, "S")
-            nn(s, 0)
-            xcp(s + 2, 0, "S")
-            actl(s, "g", 1)
-            yy(s - 1)
-            actl(s, "h", 1)
-            store(out_1, "nht", s - 1, None)
-            store(out_0, "y", s - 1, None)
-            mxp(s, 1)
-            dd(s, 1)
-            xt(s + 2, 1)
-            if s < 5:
-                xr(s + 3, 0, "S")
-            actl(s, "f", 1)
-            xcp(s + 2, 1, "S")
-            xt(s + 2, 2)
-            pbias(s, 0)
-            ee(s, 1)
-            xt(s + 2, 3)
-            pbias(s, 1)
-            xcp(s + 2, 2, "S")
-            nn(s, 1)
-            xcp(s + 2, 3, "S")
+        load_x(7)
+        actl(2, "g", 0)
+        pbias(0, 1)
+        actl(2, "h", 0)
+        pbias(1, 1)
+        mxl(2, "f", 0)
+        nt(1, 0)
+        nt(1, 1)
+        xt(4, 0)
+        actl(2, "f", 0)
+        mxl(2, "g", 1)
+        yy(0)
+        ncp(1, 0, "S")
+        store(out_1, "nht", 0, None)
+        mxl(2, "h", 1)
+        store(out_0, "y", 0, None)
+        ncp(1, 1, "S")
+        store(out_1, "nht", 1, None)
+        mxl(2, "f", 1)
+        xr(4, 1, "V")
+        xcp(4, 0, "S")
+        xqz(3)
+        mxp(2, 0)
+        actl(2, "g", 1)
+        mxp(2, 1)
+        actl(2, "h", 1)
+        dd(2, 0)
+        xt(4, 1)
+        actl(2, "f", 1)
+        xr(4, 2, "V")
+        xt(4, 2)
+        xt(4, 3)
+        ee(2, 0)
+        xcp(4, 1, "S")
+        mxl(3, "g", 0)
+        nn(2, 0)
+        xcp(4, 2, "S")
+        mxl(3, "h", 0)
+        yy(1)
+        store(out_0, "y", 1, None)
+        xcp(4, 3, "S")
+        actl(3, "g", 0)
+        dd(2, 1)
+        actl(3, "h", 0)
+        pbias(2, 0)
+        mxl(3, "f", 0)
+        xr(5, 3, "S")
+        actl(3, "f", 0)
+        ee(2, 1)
+        pbias(2, 1)
+        nn(2, 1)
+        nt(2, 0)
+        nt(2, 1)
+        xt(5, 0)
+        mxl(3, "g", 1)
+        mxl(3, "h", 1)
+        ncp(2, 0, "S")
+        mxl(3, "f", 1)
+        ncp(2, 1, "S")
+        store(out_1, "nht", 2, None)
+        mxp(3, 0)
+        xcp(5, 0, "S")
+        xr(5, 1, "V")
+        xqz(4)
+        actl(3, "g", 1)
+        mxp(3, 1)
+        xt(5, 1)
+        actl(3, "h", 1)
+        dd(3, 0)
+        xr(6, 0, "S")
+        actl(3, "f", 1)
+        xr(5, 2, "V")
+        xt(5, 2)
+        xt(5, 3)
+        mxl(4, "g", 0)
+        mxl(4, "h", 0)
+        ee(3, 0)
+        xcp(5, 1, "S")
+        nn(3, 0)
+        xcp(5, 2, "S")
+        yy(2)
+        store(out_0, "y", 2, None)
+        xcp(5, 3, "S")
+        actl(4, "g", 0)
+        dd(3, 1)
+        actl(4, "h", 0)
+        pbias(3, 0)
+        mxl(4, "f", 0)
+        xr(6, 3, "S")
+        actl(4, "f", 0)
+        ee(3, 1)
+        pbias(3, 1)
+        nn(3, 1)
+        nt(3, 0)
+        nt(3, 1)
+        xt(6, 0)
+        mxl(4, "g", 1)
+        mxl(4, "h", 1)
+        mxl(4, "f", 1)
+        mxp(4, 0)
+        ncp(3, 0, "S")
+        ncp(3, 1, "S")
+        store(out_1, "nht", 3, None)
+        xcp(6, 0, "S")
+        xr(6, 1, "V")
+        xqz(5)
+        actl(4, "g", 1)
+        mxp(4, 1)
+        xt(6, 1)
+        actl(4, "h", 1)
+        dd(4, 0)
+        xr(7, 0, "S")
+        actl(4, "f", 1)
+        xr(6, 2, "V")
+        xt(6, 2)
+        xt(6, 3)
+        mxl(5, "g", 0)
+        mxl(5, "h", 0)
+        ee(4, 0)
+        xcp(6, 1, "S")
+        nn(4, 0)
+        xcp(6, 2, "S")
+        yy(3)
+        store(out_0, "y", 3, None)
+        xcp(6, 3, "S")
+        actl(5, "g", 0)
+        dd(4, 1)
+        actl(5, "h", 0)
+        pbias(4, 0)
+        mxl(5, "f", 0)
+        xr(7, 3, "S")
+        actl(5, "f", 0)
+        ee(4, 1)
+        pbias(4, 1)
+        nn(4, 1)
+        nt(4, 0)
+        nt(4, 1)
+        xt(7, 0)
+        mxl(5, "g", 1)
+        mxl(5, "h", 1)
+        mxl(5, "f", 1)
+        mxp(5, 0)
+        ncp(4, 0, "S")
+        ncp(4, 1, "S")
+        store(out_1, "nht", 4, None)
+        xcp(7, 0, "S")
+        xr(7, 1, "V")
+        xqz(6)
+        actl(5, "g", 1)
+        mxp(5, 1)
+        xt(7, 1)
+        actl(5, "h", 1)
+        dd(5, 0)
+        actl(5, "f", 1)
+        xr(7, 2, "V")
+        xt(7, 2)
+        xt(7, 3)
         mxl(6, "g", 0)
         mxl(6, "h", 0)
-        mxl(6, "f", 0)
+        xcp(7, 1, "S")
+        ee(5, 0)
+        xcp(7, 2, "S")
+        nn(5, 0)
+        xcp(7, 3, "S")
+        yy(4)
+        store(out_0, "y", 4, None)
         actl(6, "g", 0)
+        actl(6, "h", 0)
+        dd(5, 1)
+        pbias(5, 0)
+        mxl(6, "f", 0)
+        actl(6, "f", 0)
+        ee(5, 1)
+        pbias(5, 1)
+        nn(5, 1)
         nt(5, 0)
         nt(5, 1)
-        xqz(7)
-        actl(6, "h", 0)
-        dd(6, 0)
-        actl(6, "f", 0)
         mxl(6, "g", 1)
         mxl(6, "h", 1)
-        ee(6, 0)
-        ncp(5, 0, "S")
         mxl(6, "f", 1)
         mxp(6, 0)
+        ncp(5, 0, "S")
         ncp(5, 1, "S")
-        nn(6, 0)
-        actl(6, "g", 1)
-        yy(5)
-        actl(6, "h", 1)
         store(out_1, "nht", 5, None)
-        store(out_0, "y", 5, None)
+        actl(6, "g", 1)
         mxp(6, 1)
-        dd(6, 1)
+        actl(6, "h", 1)
+        xqz(7)
+        mxl(7, "g", 0)
         actl(6, "f", 1)
+        mxl(7, "h", 0)
+        actl(7, "g", 0)
+        dd(6, 0)
+        actl(7, "h", 0)
+        ee(6, 0)
+        nn(6, 0)
+        yy(5)
+        store(out_0, "y", 5, None)
+        dd(6, 1)
         pbias(6, 0)
+        mxl(7, "f", 0)
+        actl(7, "f", 0)
         ee(6, 1)
         pbias(6, 1)
         nn(6, 1)
-        mxl(7, "h", 0)
-        mxl(7, "g", 0)
-        mxl(7, "f", 0)
-        actl(7, "h", 0)
         nt(6, 0)
         nt(6, 1)
         mxl(7, "g", 1)
-        actl(7, "g", 0)
-        actl(7, "f", 0)
-        ncp(6, 1, "S")
-        dd(7, 0)
         mxl(7, "h", 1)
-        actl(7, "g", 1)
-        ncp(6, 0, "V")
         mxl(7, "f", 1)
+        mxp(7, 0)
+        ncp(6, 0, "S")
+        ncp(6, 1, "S")
+        store(out_1, "nht", 6, None)
+        actl(7, "g", 1)
+        mxp(7, 1)
         actl(7, "h", 1)
+        actf2(7, 2)
+        actf2(7, 3)
+        dd(7, 0)
         ee(7, 0)
         yy(6)
-        actf2(7, 2)
-        dd(7, 1)
+        store(out_0, "y", 6, None)
         nn(7, 0)
-        mxp(7, 0)
-        actf2(7, 3)
+        dd(7, 1)
         ee2(7, 2)
         ee2(7, 3)
-        mxp(7, 1)
         nn2(7, 2)
         nt(7, 0)
-        nn2(7, 3)
-        store(out_1, "nht", 6, None)
-        store(out_0, "y", 6, None)
-        pbias(7, 0)
-        nt(7, 1)
         ncp(7, 0, "S")
+        store(out_1, "nht", 7, 0)
+        nn2(7, 3)
+        nt(7, 1)
         ncp(7, 1, "S")
+        store(out_1, "nht", 7, 1)
+        pbias(7, 0)
         pbias(7, 1)
         yh(7, 0)
-        store(out_1, "nht", 7, 0)
-        store(out_1, "nht", 7, 1)
-        store(out_0, "y", 7, 0)
         yh(7, 1)
+        store(out_0, "y", 7, 0)
         store(out_0, "y", 7, 1)

@@ -12,730 +12,625 @@ ALU = mybir.AluOpType
 ACT = mybir.ActivationFunctionType
 
 P = 128
-B, IN_F, N_HID = 4096, 768, 256
+TOKENS, IN_F, N_HID = 4096, 768, 256
 K = IN_F + N_HID
-SB = 512
-JT = SB // P
-NSB = B // SB
-FLOPS = 2 * B * K * 5 * N_HID
+ROUND = 512
+TILES = ROUND // P
+ROUNDS = TOKENS // ROUND
+PASSES = K // 512
+MX_ALIGN = 64
+FLOPS = 2 * TOKENS * K * 5 * N_HID
 
 
 def tile_ncpliquidcell_t_kernel(
     tc, x, hidden, mask, Wg, bg, Wh, bh, Wfg, bfg, Wfh, bfh, Wp, bp, out_0, out_1
 ):
     nc = tc.nc
+    on_scalar, on_vector = nc.scalar.copy, nc.vector.tensor_copy
     weights = [Wg, Wh, Wfg, Wfh, Wp]
+    WP = 4
+    layers = {"g": [0], "h": [1], "f": [2, 3]}
+
     with ExitStack() as ctx:
         const = ctx.enter_context(tc.tile_pool(name="const", bufs=1))
-        wraw = ctx.enter_context(tc.tile_pool(name="wraw", bufs=10))
-        wgr = ctx.enter_context(tc.tile_pool(name="wgr", bufs=2))
-        xin = ctx.enter_context(tc.tile_pool(name="xin", bufs=NSB - 2))
-        xre = ctx.enter_context(tc.tile_pool(name="xre", bufs=6))
-        xgr = ctx.enter_context(tc.tile_pool(name="xgr", bufs=2))
-        xq = ctx.enter_context(tc.tile_pool(name="xq", bufs=3))
-        act = ctx.enter_context(tc.tile_pool(name="act", bufs=3))
-        ep = ctx.enter_context(tc.tile_pool(name="ep", bufs=2))
-        outp = ctx.enter_context(tc.tile_pool(name="outp", bufs=3))
-        tr = ctx.enter_context(tc.psum_pool(name="tr", bufs=4))
-        mx = ctx.enter_context(tc.psum_pool(name="mx", bufs=4))
+        w_pool = ctx.enter_context(tc.tile_pool(name="w", bufs=10))
+        w_grouped_pool = ctx.enter_context(tc.tile_pool(name="w_grouped", bufs=2))
+        x_pool = ctx.enter_context(tc.tile_pool(name="x", bufs=ROUNDS - 2))
+        sorted_pool = ctx.enter_context(tc.tile_pool(name="sorted", bufs=6))
+        x_grouped_pool = ctx.enter_context(tc.tile_pool(name="x_grouped", bufs=2))
+        x_codes_pool = ctx.enter_context(tc.tile_pool(name="x_codes", bufs=3))
+        tanh_pool = ctx.enter_context(tc.tile_pool(name="tanh", bufs=3))
+        blend_pool = ctx.enter_context(tc.tile_pool(name="blend", bufs=2))
+        y_features_pool = ctx.enter_context(tc.tile_pool(name="y_features", bufs=1))
+        out_pool = ctx.enter_context(tc.tile_pool(name="out", bufs=3))
+        tr_pool = ctx.enter_context(tc.psum_pool(name="tr", bufs=4))
+        mx_pool = ctx.enter_context(tc.psum_pool(name="mx", bufs=4))
         ctx.enter_context(tc.manual_schedule())
 
-        ones_bf = const.tile([P, P], BF16)
-        nc.vector.memset(ones_bf[:], 1.0)
-        dz = const.tile([P, 512], BF16)
-        nc.vector.memset(dz[:], 0.0)
-        zt_bf = const.tile([P, P], BF16)
-        nc.vector.memset(zt_bf[:], 0.0)
-        zb_bf = const.tile([P, N_HID], BF16)
-        nc.vector.memset(zb_bf[:], 0.0)
-        warm = const.tile([P, 1], F32)
-        nc.vector.memset(warm[:], 0.0)
-        warm2 = const.tile([P, 1], F32)
-        nc.scalar.activation(out=warm2[:], in_=warm[:], func=ACT.Tanh)
-        ident = const.tile([P, P], F32)
-        make_identity(nc, ident[:])
+        ones = const.tile([P, P], BF16, name="ones")
+        nc.vector.memset(ones[:], 1.0)
+        zeros = const.tile([P, 512], BF16, name="zeros")
+        nc.vector.memset(zeros[:], 0.0)
+        bias_rows = const.tile([P, P], BF16, name="bias_rows")
+        nc.vector.memset(bias_rows[:], 0.0)
+        bp_row = const.tile([P, N_HID], BF16, name="bp_row")
+        nc.vector.memset(bp_row[:], 0.0)
+        zero_col = const.tile([P, 1], F32, name="zero_col")
+        nc.vector.memset(zero_col[:], 0.0)
+        tanh_col = const.tile([P, 1], F32, name="tanh_col")
+        nc.scalar.activation(out=tanh_col[:], in_=zero_col[:], func=ACT.Tanh)
+        identity = const.tile([P, P], F32, name="identity")
+        make_identity(nc, identity[:])
         for i, b in enumerate([bg, bh, bfg, bfh]):
-            nc.gpsimd.dma_start(out=zt_bf[2 * i : 2 * i + 2, :], in_=b.rearrange("(r c) -> r c", r=2))
-        nc.gpsimd.dma_start(out=zb_bf[0:1, :], in_=bp.rearrange("(o c) -> o c", o=1))
+            nc.gpsimd.dma_start(out=bias_rows[2 * i : 2 * i + 2, :], in_=b.rearrange("(r c) -> r c", r=2))
+        nc.gpsimd.dma_start(out=bp_row[0:1, :], in_=bp.rearrange("(o c) -> o c", o=1))
 
-        mask_sb = [const.tile([P, K], BF16, name="mask%d" % hf) for hf in range(2)]
-        w_sb = [[wraw.tile([P, K], BF16, name="w%d_%d" % (w, hf), tag="w") for hf in range(2)] for w in range(5)]
+        mask_sb = [const.tile([P, K], BF16, name="mask%d" % h) for h in range(2)]
+        w_sb = [[w_pool.tile([P, K], BF16, name="w%d_%d" % (w, h), tag="w") for h in range(2)] for w in range(5)]
+
+        bias_words = const.tile([P, P], F32, name="bias_words")
+        bias_cols = const.tile([P, 8], F32, name="bias_cols")
+        gate_sum = const.tile([P, 2], F32, name="gate_sum")
+        gate_bias = const.tile([P, 2], F32, name="gate_bias")
+        bp_spread = const.tile([P, 2, N_HID], F32, name="bp_spread")
+        bp_cols = const.tile([P, 2], F32, name="bp_cols")
+
+        w_codes = [const.tile([P, 2, PASSES, P], U32, name="w_codes%d" % w, align_bytes=MX_ALIGN) for w in range(WP)]
+        w_scales = [const.tile([P, 2, PASSES, P], U8, name="w_scales%d" % w, align_bytes=MX_ALIGN) for w in range(WP)]
+        w_codes.append(const.tile([P, PASSES, N_HID], U32, name="w_codes4", align_bytes=MX_ALIGN))
+        w_scales.append(const.tile([P, PASSES, N_HID], U8, name="w_scales4", align_bytes=MX_ALIGN))
+
+        tiles = {}
         x_sb = {}
 
-        def load_m(hf):
-            nc.sync.dma_start(out=mask_sb[hf][:], in_=mask[P * hf : P * (hf + 1), :])
 
-        def load_w(w, hf):
-            nc.sync.dma_start(out=w_sb[w][hf][:], in_=weights[w][P * hf : P * (hf + 1), :])
+        def load_mask(h):
+            nc.sync.dma_start(out=mask_sb[h][:], in_=mask[P * h : P * (h + 1), :])
 
-        def load_x(s):
-            rows = slice(SB * s, SB * (s + 1))
-            x_sb[s] = xin.tile([P, JT, K], BF16, name="x", tag="x")
-            nc.sync.dma_start(out=x_sb[s][:, :, 0:IN_F], in_=x[rows, :].rearrange("(p j) k -> p j k", j=JT))
-            nc.sync.dma_start(out=x_sb[s][:, :, IN_F:K], in_=hidden[rows, :].rearrange("(p j) k -> p j k", j=JT))
+        def load_weight(w, h):
+            nc.sync.dma_start(out=w_sb[w][h][:], in_=weights[w][P * h : P * (h + 1), :])
+
+        def load_rows(r):
+            rows = slice(ROUND * r, ROUND * (r + 1))
+            x_sb[r] = x_pool.tile([P, TILES, K], BF16, name="x_rows", tag="x")
+            nc.sync.dma_start(out=x_sb[r][:, :, 0:IN_F], in_=x[rows, :].rearrange("(q j) k -> q j k", j=TILES))
+            nc.sync.dma_start(out=x_sb[r][:, :, IN_F:K], in_=hidden[rows, :].rearrange("(q j) k -> q j k", j=TILES))
 
 
-        def load_xh(s, h):
-            js = slice(2 * h, 2 * h + 2)
-            if s not in x_sb:
-                x_sb[s] = xin.tile([P, JT, K], BF16, name="x", tag="x")
-            for src, cols in ((x, slice(0, IN_F)), (hidden, slice(IN_F, K))):
-                view = src[SB * s : SB * (s + 1), :].rearrange("(p j) k -> p j k", j=JT)
-                nc.sync.dma_start(out=x_sb[s][:, js, cols], in_=view[:, js, :])
+        def dummy_matmuls(count):
+            if "dummy" not in tiles:
+                tiles["dummy"] = mx_pool.tile([P, 512], F32, tag="mx", name="dummy")
+            for i in range(count):
+                nc.tensor.matmul(out=tiles["dummy"][:], lhsT=ones[:], rhs=zeros[:], start=True, stop=True)
 
-        zt = const.tile([P, P], F32)
-        bias_sb = const.tile([P, 8], F32)
-        bf_sum = const.tile([P, 2], F32)
-        bf_half = const.tile([P, 2], F32)
-        bp_bc = const.tile([P, 2, N_HID], F32)
-        t = {}
+        def prepare_biases():
+            nc.vector.tensor_copy(out=bias_words[:], in_=bias_rows[:])
 
-        def dm():
-            if "dm" not in t:
-                t["dm"] = mx.tile([P, 512], F32, tag="mx", name="dmb")
-            nc.tensor.matmul(out=t["dm"][:], lhsT=ones_bf[:], rhs=dz[:], start=True, stop=True)
+        def transpose_biases():
+            bank = mx_pool.tile([P, 512], F32, tag="mx", name="bias_bank")
+            tiles["bias"] = bank
+            nc.tensor.transpose(bank[:, 0:P], bias_words[:], identity[:])
+            nc.tensor.matmul(out=bank[:, P : P + N_HID], lhsT=ones[:], rhs=bp_row[:], start=True, stop=True)
 
-        def bc():
-            nc.vector.tensor_copy(out=zt[:], in_=zt_bf[:])
+        def finish_biases():
+            nc.vector.tensor_copy(out=bias_cols[:], in_=tiles["bias"][:, 0:8])
+            nc.vector.tensor_tensor(out=gate_sum[:], in0=bias_cols[:, 4:6], in1=bias_cols[:, 6:8], op=ALU.add)
+            nc.vector.tensor_scalar_mul(out=gate_bias[:], in0=gate_sum[:], scalar1=0.5)
 
-        def bt():
-            t["bt"] = mx.tile([P, 512], F32, tag="mx", name="bt")
-            nc.tensor.transpose(t["bt"][:, 0:P], zt[:], ident[:])
-            nc.tensor.matmul(out=t["bt"][:, P : P + N_HID], lhsT=ones_bf[:], rhs=zb_bf[:], start=True, stop=True)
+        def spread_bp():
+            for i in range(2):
+                on_scalar(out=bp_spread[:, i, :], in_=tiles["bias"][:, P : P + N_HID])
 
-        def bv():
-            nc.vector.tensor_copy(out=bias_sb[:], in_=t["bt"][:, 0:8])
-            nc.vector.tensor_tensor(out=bf_sum[:], in0=bias_sb[:, 4:6], in1=bias_sb[:, 6:8], op=ALU.add)
-            nc.vector.tensor_scalar_mul(out=bf_half[:], in0=bf_sum[:], scalar1=0.5)
+        def transpose_bp():
+            tiles["bp"] = mx_pool.tile([P, 512], F32, tag="mx", name="bp_bank")
+            for h in range(2):
+                cols = slice(P * h, P * (h + 1))
+                nc.tensor.transpose(tiles["bp"][:, cols], bp_spread[:, 0, cols], identity[:])
 
-        def bw(eng):
-            for r in range(2):
-                copy_on(eng, bp_bc[:, r, :], t["bt"][:, P : P + N_HID])
+        def finish_bp():
+            nc.vector.tensor_copy(out=bp_cols[:], in_=tiles["bp"][:, 0 : 2 * P : P])
 
-        wc = [const.tile([P, 2, 2, P], U32, name="wc%d" % w, align_bytes=64) for w in range(4)]
-        ws = [const.tile([P, 2, 2, P], U8, name="ws%d" % w, align_bytes=64) for w in range(4)]
-        wc.append(const.tile([P, 2, N_HID], U32, name="wc4", align_bytes=64))
-        ws.append(const.tile([P, 2, N_HID], U8, name="ws4", align_bytes=64))
 
-        def copy_on(eng, out, in_):
-            if eng == "S":
-                nc.scalar.copy(out=out, in_=in_)
+        def transpose_words(words):
+            bank = tr_pool.tile([P, 512], F32, tag="tr", name="words")
+            for g in range(PASSES):
+                for u in range(2):
+                    o = P * (2 * g + u)
+                    nc.tensor.transpose(bank[:, o : o + P], words(g, u), identity[:])
+            return bank
+
+        def every_second(row_words):
+            return lambda g, u: row_words[:, 256 * g + u : 256 * (g + 1) : 2]
+
+        def gather(copy, out, bank):
+            copy(out=out, in_=bank[:].rearrange("q (g u c) -> q g c u", g=PASSES, u=2))
+
+
+        def mask_weight(w, h):
+            nc.vector.tensor_tensor(out=w_sb[w][h][:], in0=w_sb[w][h][:], in1=mask_sb[h][:], op=ALU.mult)
+
+        def transpose_weight(w, h):
+            tiles["w_words", w, h] = transpose_words(every_second(w_sb[w][h][:].bitcast(F32)))
+
+        def gather_weight(w, h, copy):
+            if ("w_grouped", w) not in tiles:
+                tiles["w_grouped", w] = w_grouped_pool.tile(
+                    [P, 2, PASSES, P, 2], F32, tag="w_grouped", name="w_grouped", align_bytes=MX_ALIGN
+                )
+            grouped = tiles["w_grouped", w]
+            if w == WP:
+                part = grouped[:].rearrange("q a b c u -> q a (b c) u")[:, :, P * h : P * (h + 1), :]
             else:
-                nc.vector.tensor_copy(out=out, in_=in_)
+                part = grouped[:, h, :, :, :]
+            gather(copy, part, tiles["w_words", w, h])
 
-        def mm(w, hf):
-            nc.vector.tensor_tensor(out=w_sb[w][hf][:], in0=w_sb[w][hf][:], in1=mask_sb[hf][:], op=ALU.mult)
+        def quantize_half(w, h):
+            nc.vector.quantize_mx(
+                out=w_codes[w][:, h, :, :].rearrange("q g c -> q (g c)").bitcast(FP8X4),
+                scales=w_scales[w][:, h, :, :].rearrange("q g c -> q (g c)"),
+                in_=tiles["w_grouped", w][:, h, :, :, :].rearrange("q g c u -> q (g c u)").bitcast(BF16),
+            )
 
-        def wt(w, hf):
-            bank = tr.tile([P, 512], F32, tag="tr", name="wt")
-            t["wt", w, hf] = bank
-            ww = w_sb[w][hf][:].bitcast(F32)
-            for b in range(4):
-                nc.tensor.transpose(bank[:, P * b : P * (b + 1)], ww[:, 2 * P * (b // 2) + b % 2 : 2 * P * (b // 2 + 1) : 2], ident[:])
+        def quantize_wp():
+            nc.vector.quantize_mx(
+                out=w_codes[WP][:].rearrange("q g c -> q (g c)").bitcast(FP8X4),
+                scales=w_scales[WP][:].rearrange("q g c -> q (g c)"),
+                in_=tiles["w_grouped", WP][:].rearrange("q a b c u -> q (a b c u)").bitcast(BF16),
+            )
 
-        def wcp(w, hf, eng):
-            if ("wg", w) not in t:
-                t["wg", w] = wgr.tile([P, 2, 2, P, 2], F32, tag="wg", name="wg", align_bytes=64)
-            if w < 4:
-                dst = t["wg", w][:, hf, :, :, :]
+
+        def sort_words(r, j, copy):
+            tiles["sorted", r, j] = sorted_pool.tile([P, PASSES, 2, P], F32, tag="sorted", name="sorted_words")
+            copy(
+                out=tiles["sorted", r, j][:],
+                in_=x_sb[r][:, j, :].bitcast(F32).rearrange("q (g c u) -> q g u c", g=PASSES, u=2),
+            )
+
+        def transpose_tile(r, j):
+            if ("sorted", r, j) in tiles:
+                in_order = tiles["sorted", r, j]
+                tiles["x_words", r, j] = transpose_words(lambda g, u: in_order[:, g, u, :])
             else:
-                dst = t["wg", w][:].rearrange("q a b c u -> q a (b c) u")[:, :, P * hf : P * (hf + 1), :]
-            copy_on(eng, dst, t["wt", w, hf][:].rearrange("q (g u c) -> q g c u", g=2, u=2))
+                tiles["x_words", r, j] = transpose_words(every_second(x_sb[r][:, j, :].bitcast(F32)))
 
-        def wq(w):
+        def gather_tile(r, j, copy):
+            if ("x_grouped", r) not in tiles:
+                tiles["x_grouped", r] = x_grouped_pool.tile(
+                    [P, PASSES, ROUND, 2], F32, tag="x_grouped", name="x_grouped", align_bytes=MX_ALIGN
+                )
+            gather(copy, tiles["x_grouped", r][:, :, P * j : P * (j + 1), :], tiles["x_words", r, j])
+
+        def quantize_rows(r):
+            tiles["x_codes", r] = x_codes_pool.tile([P, PASSES, ROUND], U32, tag="codes", name="x_codes", align_bytes=MX_ALIGN)
+            tiles["x_scales", r] = x_codes_pool.tile([P, PASSES, ROUND], U8, tag="scales", name="x_scales", align_bytes=MX_ALIGN)
             nc.vector.quantize_mx(
-                out=wc[w][:].rearrange("q g c -> q (g c)").bitcast(FP8X4),
-                scales=ws[w][:].rearrange("q g c -> q (g c)"),
-                in_=t["wg", w][:].rearrange("q a b c u -> q (a b c u)").bitcast(BF16),
+                out=tiles["x_codes", r][:].rearrange("q g c -> q (g c)").bitcast(FP8X4),
+                scales=tiles["x_scales", r][:].rearrange("q g c -> q (g c)"),
+                in_=tiles["x_grouped", r][:].rearrange("q g c u -> q (g c u)").bitcast(BF16),
             )
 
-        def wh(w, hf):
-            nc.vector.quantize_mx(
-                out=wc[w][:, hf, :, :].rearrange("q g c -> q (g c)").bitcast(FP8X4),
-                scales=ws[w][:, hf, :, :].rearrange("q g c -> q (g c)"),
-                in_=t["wg", w][:, hf, :, :, :].rearrange("q g c u -> q (g c u)").bitcast(BF16),
-            )
 
-        def xr(s, j, eng):
-            t["xr", s, j] = xre.tile([P, 2, 2, P], F32, tag="xr", name="xr")
-            copy_on(eng, t["xr", s, j][:], x_sb[s][:, j, :].bitcast(F32).rearrange("q (g c u) -> q g u c", g=2, u=2))
+        def add_up(bank, weight_views, r):
+            passes = [(codes, scales, g) for codes, scales in weight_views for g in range(PASSES)]
+            for i, (codes, scales, g) in enumerate(passes):
+                nc.tensor.matmul_mx(
+                    out=bank[:],
+                    lhsT=codes(g).bitcast(FP8X4),
+                    lhsT_scale=scales(g),
+                    rhs=tiles["x_codes", r][:, g, :].bitcast(FP8X4),
+                    rhs_scale=tiles["x_scales", r][:, g, :],
+                    start=(i == 0),
+                    stop=(i == len(passes) - 1),
+                )
 
-        def xt(s, j):
-            bank = tr.tile([P, 512], F32, tag="tr", name="xt")
-            t["xt", s, j] = bank
-            xw = x_sb[s][:, j, :].bitcast(F32)
-            for b in range(4):
-                if ("xr", s, j) in t:
-                    words = t["xr", s, j][:, b // 2, b % 2, :]
-                else:
-                    words = xw[:, 256 * (b // 2) + b % 2 : 256 * (b // 2 + 1) : 2]
-                nc.tensor.transpose(bank[:, P * b : P * (b + 1)], words, ident[:])
+        def multiply(r, layer, h):
+            bank = mx_pool.tile([P, 512], F32, tag="mx", name="layer")
+            tiles[layer, r, h] = bank
+            views = [
+                (lambda g, w=w: w_codes[w][:, h, g, :], lambda g, w=w: w_scales[w][:, h, g, :]) for w in layers[layer]
+            ]
+            add_up(bank, views, r)
 
-        def xcp(s, j, eng):
-            if ("xg", s) not in t:
-                t["xg", s] = xgr.tile([P, 2, SB, 2], F32, tag="xg", name="xg", align_bytes=64)
-            copy_on(
-                eng,
-                t["xg", s][:, :, P * j : P * (j + 1), :],
-                t["xt", s, j][:].rearrange("q (g u c) -> q g c u", g=2, u=2),
-            )
+        def multiply_p_features(r, h):
+            bank = mx_pool.tile([P, 512], F32, tag="mx", name="p_features")
+            tiles["p_features", r, h] = bank
+            cols = slice(P * h, P * (h + 1))
+            add_up(bank, [(lambda g: w_codes[WP][:, g, cols], lambda g: w_scales[WP][:, g, cols])], r)
 
-        def xqz(s):
-            t["xc", s] = xq.tile([P, 2, SB], U32, tag="xc", name="xc", align_bytes=64)
-            t["xs", s] = xq.tile([P, 2, SB], U8, tag="xs", name="xs", align_bytes=64)
-            nc.vector.quantize_mx(
-                out=t["xc", s][:].rearrange("q g c -> q (g c)").bitcast(FP8X4),
-                scales=t["xs", s][:].rearrange("q g c -> q (g c)"),
-                in_=t["xg", s][:].rearrange("q g c u -> q (g c u)").bitcast(BF16),
-            )
-
-        layers = {"g": [0], "h": [1], "f": [2, 3]}
-
-        def mxl(s, lay, hf):
-            acc = mx.tile([P, 512], F32, tag="mx", name="acc")
-            t["acc", s, lay, hf] = acc
-            wlist = layers[lay]
-            n = 2 * len(wlist)
-            i = 0
-            for w in wlist:
-                for g in range(2):
+        def multiply_p(r, p):
+            bank = mx_pool.tile([P, 512], F32, tag="mx", name="p_tokens")
+            tiles["p", r, p] = bank
+            for i in range(2):
+                cols = slice(P * (2 * p + i), P * (2 * p + i + 1))
+                for g in range(PASSES):
                     nc.tensor.matmul_mx(
-                        out=acc[:],
-                        lhsT=wc[w][:, hf, g, :].bitcast(FP8X4),
-                        lhsT_scale=ws[w][:, hf, g, :],
-                        rhs=t["xc", s][:, g, :].bitcast(FP8X4),
-                        rhs_scale=t["xs", s][:, g, :],
-                        start=(i == 0),
-                        stop=(i == n - 1),
-                    )
-                    i += 1
-
-        def actl(s, lay, hf):
-            if (lay, s) not in t:
-                t[lay, s] = act.tile([P, 2, SB], F32, tag=lay, name="a" + lay)
-            if lay == "g":
-                bias, scale = bias_sb[:, hf : hf + 1], 1.0
-            elif lay == "h":
-                bias, scale = bias_sb[:, 2 + hf : 3 + hf], 1.0
-            else:
-                bias, scale = bf_half[:, hf : hf + 1], 0.5
-            nc.scalar.activation(out=t[lay, s][:, hf, :], in_=t["acc", s, lay, hf][:], func=ACT.Tanh, bias=bias, scale=scale)
-
-        def actf2(s, k):
-            hf, c = k // 2, k % 2
-            cols = slice(N_HID * c, N_HID * (c + 1))
-            if ("f", s) not in t:
-                t["f", s] = act.tile([P, 2, SB], F32, tag="f", name="af")
-            nc.scalar.activation(
-                out=t["f", s][:, hf, cols], in_=t["acc", s, "f", hf][:, cols], func=ACT.Tanh, bias=bf_half[:, hf : hf + 1], scale=0.5
-            )
-
-        def ee2(s, k):
-            hf, c = k // 2, k % 2
-            cols = slice(N_HID * c, N_HID * (c + 1))
-            nc.vector.scalar_tensor_tensor(
-                out=t["d", s][:, hf, cols], in0=t["f", s][:, hf, cols], scalar=1.0, in1=t["d", s][:, hf, cols], op0=ALU.add, op1=ALU.mult
-            )
-
-        def nn2(s, k):
-            hf, c = k // 2, k % 2
-            cols = slice(N_HID * c, N_HID * (c + 1))
-            if ("nh", s) not in t:
-                t["nh", s] = ep.tile([P, 2, SB], F32, tag="nh", name="nh")
-            nc.vector.scalar_tensor_tensor(
-                out=t["nh", s][:, hf, cols], in0=t["d", s][:, hf, cols], scalar=0.5, in1=t["g", s][:, hf, cols], op0=ALU.mult, op1=ALU.add
-            )
-
-        def mxp(s, jp):
-            acc = mx.tile([P, 512], F32, tag="mx", name="accp")
-            t["accp", s, jp] = acc
-            for jj in range(2):
-                cols = slice(P * (2 * jp + jj), P * (2 * jp + jj + 1))
-                for g in range(2):
-                    nc.tensor.matmul_mx(
-                        out=acc[:, N_HID * jj : N_HID * (jj + 1)],
-                        lhsT=t["xc", s][:, g, cols].bitcast(FP8X4),
-                        lhsT_scale=t["xs", s][:, g, cols],
-                        rhs=wc[4][:, g, :].bitcast(FP8X4),
-                        rhs_scale=ws[4][:, g, :],
+                        out=bank[:, N_HID * i : N_HID * (i + 1)],
+                        lhsT=tiles["x_codes", r][:, g, cols].bitcast(FP8X4),
+                        lhsT_scale=tiles["x_scales", r][:, g, cols],
+                        rhs=w_codes[WP][:, g, :].bitcast(FP8X4),
+                        rhs_scale=w_scales[WP][:, g, :],
                         start=(g == 0),
-                        stop=(g == 1),
+                        stop=(g == PASSES - 1),
                     )
 
-        def half(tile_, jp):
-            return tile_[:, 2 * jp : 2 * jp + 2, :].rearrange("p a f -> p (a f)")
 
-        def pbias(s, jp):
-            if ("pb", s) not in t:
-                t["pb", s] = outp.tile([P, JT, N_HID], F32, tag="pb", name="pb")
+        def tile_of(pool, what, r, name):
+            if (what, r) not in tiles:
+                tiles[what, r] = pool.tile([P, 2, ROUND], F32, tag=what, name=name)
+            return tiles[what, r]
+
+        bias_of = {"g": (bias_cols, 0, 1.0), "h": (bias_cols, 2, 1.0), "f": (gate_bias, 0, 0.5)}
+        every = slice(0, ROUND)
+
+        def activate(r, layer, h, tokens=every):
+            cols, first, scale = bias_of[layer]
+            nc.scalar.activation(
+                out=tile_of(tanh_pool, "tanh_" + layer, r, "tanh")[:, h, tokens],
+                in_=tiles[layer, r, h][:, tokens],
+                func=ACT.Tanh,
+                bias=cols[:, first + h : first + h + 1],
+                scale=scale,
+            )
+
+        def difference(r, h):
             nc.vector.tensor_tensor(
-                out=half(t["pb", s], jp), in0=t["accp", s, jp][:], in1=bp_bc[:].rearrange("p a f -> p (a f)"), op=ALU.add
+                out=tile_of(blend_pool, "step", r, "step")[:, h, :],
+                in0=tiles["tanh_h", r][:, h, :],
+                in1=tiles["tanh_g", r][:, h, :],
+                op=ALU.subtract,
             )
 
-        def dd(s, hf):
-            if ("d", s) not in t:
-                t["d", s] = ep.tile([P, 2, SB], F32, tag="d", name="d")
-            nc.vector.tensor_tensor(out=t["d", s][:, hf, :], in0=t["h", s][:, hf, :], in1=t["g", s][:, hf, :], op=ALU.subtract)
-
-        def ee(s, hf):
+        def weigh(r, h, tokens=every):
+            step = tiles["step", r][:, h, tokens]
             nc.vector.scalar_tensor_tensor(
-                out=t["d", s][:, hf, :], in0=t["f", s][:, hf, :], scalar=1.0, in1=t["d", s][:, hf, :], op0=ALU.add, op1=ALU.mult
+                out=step, in0=tiles["tanh_f", r][:, h, tokens], scalar=1.0, in1=step, op0=ALU.add, op1=ALU.mult
             )
 
-        def nn(s, hf):
-            if ("nh", s) not in t:
-                t["nh", s] = ep.tile([P, 2, SB], F32, tag="nh", name="nh")
+        def blend(r, h, tokens=every):
             nc.vector.scalar_tensor_tensor(
-                out=t["nh", s][:, hf, :], in0=t["d", s][:, hf, :], scalar=0.5, in1=t["g", s][:, hf, :], op0=ALU.mult, op1=ALU.add
+                out=tile_of(blend_pool, "new_hidden", r, "new_hidden")[:, h, tokens],
+                in0=tiles["step", r][:, h, tokens],
+                scalar=0.5,
+                in1=tiles["tanh_g", r][:, h, tokens],
+                op0=ALU.mult,
+                op1=ALU.add,
             )
 
-        def ddm(s):
-            t["d", s] = ep.tile([P, 2, SB], F32, tag="d", name="d")
-            nc.vector.tensor_tensor(out=t["d", s][:], in0=t["h", s][:], in1=t["g", s][:], op=ALU.subtract)
-
-        def eem(s):
+        def add_to_p_features(r, h):
             nc.vector.scalar_tensor_tensor(
-                out=t["d", s][:], in0=t["f", s][:], scalar=1.0, in1=t["d", s][:], op0=ALU.add, op1=ALU.mult
+                out=tile_of(y_features_pool, "y_features", r, "y_features")[:, h, :],
+                in0=tiles["p_features", r, h][:],
+                scalar=bp_cols[:, h : h + 1],
+                in1=tiles["new_hidden", r][:, h, :],
+                op0=ALU.add,
+                op1=ALU.add,
             )
 
-        def nnm(s):
-            t["nh", s] = ep.tile([P, 2, SB], F32, tag="nh", name="nh")
-            nc.vector.scalar_tensor_tensor(
-                out=t["nh", s][:], in0=t["d", s][:], scalar=0.5, in1=t["g", s][:], op0=ALU.mult, op1=ALU.add
+
+        def rows_tile(what, r):
+            if (what, r) not in tiles:
+                tiles[what, r] = out_pool.tile([P, TILES, N_HID], F32, tag=what, name="rows")
+            return tiles[what, r]
+
+        def pair(rows, p):
+            return rows[:, 2 * p : 2 * p + 2, :].rearrange("q a f -> q (a f)")
+
+        def transpose_back(what, r, p):
+            bank = tr_pool.tile([P, 512], F32, tag="tr", name="back")
+            tiles[what + "_back", r, p] = bank
+            for i in range(2):
+                for h in range(2):
+                    o = N_HID * i + P * h
+                    j = 2 * p + i
+                    nc.tensor.transpose(bank[:, o : o + P], tiles[what, r][:, h, P * j : P * (j + 1)], identity[:])
+
+        def copy_hidden(r, p):
+            on_scalar(out=pair(rows_tile("hidden_rows", r), p), in_=tiles["new_hidden_back", r, p][:])
+
+        def copy_y(r, p):
+            on_scalar(out=pair(rows_tile("y_rows", r), p), in_=tiles["y_features_back", r, p][:])
+
+        def add_bp(r, p):
+            nc.vector.tensor_tensor(
+                out=pair(rows_tile("p_rows", r), p),
+                in0=tiles["p", r, p][:],
+                in1=bp_spread[:].rearrange("q a f -> q (a f)"),
+                op=ALU.add,
             )
 
-        def nt(s, jp):
-            bank = tr.tile([P, 512], F32, tag="tr", name="nt")
-            t["nt", s, jp] = bank
-            for jj in range(2):
-                j = 2 * jp + jj
-                for hf in range(2):
-                    o = N_HID * jj + P * hf
-                    nc.tensor.transpose(bank[:, o : o + P], t["nh", s][:, hf, P * j : P * (j + 1)], ident[:])
+        def add_hidden(r):
+            nc.vector.tensor_tensor(
+                out=rows_tile("y_rows", r)[:], in0=tiles["hidden_rows", r][:], in1=tiles["p_rows", r][:], op=ALU.add
+            )
 
-        def ncp(s, jp, eng):
-            if ("nht", s) not in t:
-                t["nht", s] = outp.tile([P, JT, N_HID], F32, tag="nht", name="nht")
-            copy_on(eng, half(t["nht", s], jp), t["nt", s, jp][:])
+        def add_hidden_pair(r, p):
+            nc.vector.tensor_tensor(
+                out=pair(rows_tile("y_rows", r), p),
+                in0=pair(tiles["hidden_rows", r], p),
+                in1=pair(tiles["p_rows", r], p),
+                op=ALU.add,
+            )
 
-        def yh(s, jp):
-            if ("y", s) not in t:
-                t["y", s] = outp.tile([P, JT, N_HID], F32, tag="y", name="y")
-            nc.vector.tensor_tensor(out=half(t["y", s], jp), in0=half(t["nht", s], jp), in1=half(t["pb", s], jp), op=ALU.add)
+        def rows_of(dst, r):
+            return dst[ROUND * r : ROUND * (r + 1), :].rearrange("(q j) f -> q j f", j=TILES)
 
-        def yy(s):
-            t["y", s] = outp.tile([P, JT, N_HID], F32, tag="y", name="y")
-            nc.vector.tensor_tensor(out=t["y", s][:], in0=t["nht", s][:], in1=t["pb", s][:], op=ALU.add)
+        def store_round(r):
+            nc.sync.dma_start(out=rows_of(out_1, r), in_=tiles["hidden_rows", r][:])
+            nc.sync.dma_start(out=rows_of(out_0, r), in_=tiles["y_rows", r][:])
 
-        def store(dst, key, s, jp):
-            view = dst[SB * s : SB * (s + 1), :].rearrange("(p j) f -> p j f", j=JT)
-            if jp is None:
-                nc.sync.dma_start(out=view, in_=t[key, s][:])
-            else:
-                nc.sync.dma_start(out=view[:, 2 * jp : 2 * jp + 2, :], in_=t[key, s][:, 2 * jp : 2 * jp + 2, :])
+        def store_pair(dst, what, r, p):
+            js = slice(2 * p, 2 * p + 2)
+            nc.sync.dma_start(out=rows_of(dst, r)[:, js, :], in_=tiles[what, r][:, js, :])
 
-        load_x(0)
-        dm()
-        dm()
-        dm()
-        dm()
-        dm()
-        dm()
-        dm()
-        dm()
-        xt(0, 1)
-        xcp(0, 1, "S")
-        load_m(0)
-        xt(0, 3)
-        xt(0, 2)
-        xcp(0, 2, "S")
-        load_w(0, 0)
-        mm(0, 0)
-        xt(0, 0)
-        xcp(0, 0, "S")
-        xcp(0, 3, "S")
-        dm()
-        load_m(1)
-        dm()
-        load_w(0, 1)
-        mm(0, 1)
-        wt(0, 1)
-        wcp(0, 1, "S")
-        dm()
-        dm()
-        load_w(1, 0)
-        mm(1, 0)
-        xqz(0)
-        wh(0, 1)
-        wt(1, 0)
-        wcp(1, 0, "S")
-        wt(0, 0)
-        wcp(0, 0, "S")
-        load_w(1, 1)
-        mm(1, 1)
-        wh(1, 0)
-        bc()
-        wh(0, 0)
-        mxl(0, "g", 1)
-        load_x(1)
-        wt(1, 1)
-        wcp(1, 1, "S")
-        xt(1, 2)
-        xcp(1, 2, "S")
-        bt()
-        xt(1, 3)
-        mxl(0, "g", 0)
-        load_w(2, 0)
-        mm(2, 0)
-        bv()
-        actl(0, "g", 1)
-        bw("S")
-        xcp(1, 3, "V")
-        wh(1, 1)
-        xt(1, 1)
-        xt(1, 0)
-        xcp(1, 0, "S")
-        xcp(1, 1, "S")
-        actl(0, "g", 0)
-        load_w(2, 1)
-        mm(2, 1)
-        mxl(0, "h", 1)
-        load_w(3, 0)
-        mxl(0, "h", 0)
-        actl(0, "h", 0)
-        actl(0, "h", 1)
-        load_w(3, 1)
-        mm(3, 1)
-        mm(3, 0)
-        xqz(1)
-        wt(2, 0)
-        wcp(2, 0, "S")
-        wt(3, 1)
-        load_w(4, 0)
-        wt(3, 0)
-        wcp(3, 0, "V")
-        wcp(3, 1, "V")
-        load_w(4, 1)
-        wt(2, 1)
-        wh(3, 0)
-        mxl(1, "g", 0)
-        actl(1, "g", 0)
-        wcp(2, 1, "S")
-        wh(3, 1)
-        load_x(2)
-        wh(2, 0)
-        mxl(1, "h", 1)
-        actl(1, "h", 1)
-        dd(0, 0)
-        mxl(1, "g", 1)
-        actl(1, "g", 1)
-        wh(2, 1)
-        mm(4, 1)
-        mxl(1, "h", 0)
-        actl(1, "h", 0)
-        mm(4, 0)
-        mxl(0, "f", 0)
-        actl(0, "f", 0)
-        xr(2, 3, "S")
-        load_x(3)
-        dd(1, 0)
-        mxl(0, "f", 1)
-        ee(0, 0)
-        wt(4, 0)
-        wcp(4, 0, "S")
-        actl(0, "f", 1)
-        dd(0, 1)
-        wt(4, 1)
-        wcp(4, 1, "S")
-        xt(2, 0)
-        nn(0, 0)
-        xt(2, 1)
-        xcp(2, 1, "S")
-        xcp(2, 0, "S")
-        load_x(4)
-        mxl(1, "f", 0)
-        ee(0, 1)
-        actl(1, "f", 0)
-        mxl(1, "f", 1)
-        dd(1, 1)
-        actl(1, "f", 1)
-        xt(2, 3)
-        nn(0, 1)
-        xr(3, 1, "S")
-        xt(2, 2)
-        xr(3, 0, "S")
-        wq(4)
-        nt(0, 1)
-        nt(0, 0)
-        ncp(0, 0, "S")
-        load_x(5)
-        ee(1, 0)
-        mxp(0, 0)
-        ncp(0, 1, "S")
-        ee(1, 1)
-        mxp(1, 0)
-        xcp(2, 2, "S")
-        mxp(1, 1)
-        nn(1, 0)
-        xcp(2, 3, "S")
-        mxp(0, 1)
-        xr(3, 2, "V")
-        xr(4, 0, "S")
-        xr(3, 3, "V")
-        load_x(6)
-        xt(3, 1)
-        xr(4, 3, "S")
-        pbias(0, 0)
-        xt(3, 0)
-        xcp(3, 0, "S")
-        xt(3, 2)
-        nn(1, 1)
-        xt(3, 3)
-        xcp(3, 3, "S")
-        pbias(1, 0)
-        xcp(3, 1, "S")
-        xqz(2)
-        mxl(2, "g", 0)
-        mxl(2, "h", 0)
-        xcp(3, 2, "S")
-        load_x(7)
-        actl(2, "g", 0)
-        pbias(0, 1)
-        actl(2, "h", 0)
-        pbias(1, 1)
-        mxl(2, "f", 0)
-        nt(1, 0)
-        nt(1, 1)
-        xt(4, 0)
-        actl(2, "f", 0)
-        mxl(2, "g", 1)
-        yy(0)
-        ncp(1, 0, "S")
-        store(out_1, "nht", 0, None)
-        mxl(2, "h", 1)
-        store(out_0, "y", 0, None)
-        ncp(1, 1, "S")
-        store(out_1, "nht", 1, None)
-        mxl(2, "f", 1)
-        xr(4, 1, "V")
-        xcp(4, 0, "S")
-        xqz(3)
-        mxp(2, 0)
-        actl(2, "g", 1)
-        mxp(2, 1)
-        actl(2, "h", 1)
-        dd(2, 0)
-        xt(4, 1)
-        actl(2, "f", 1)
-        xr(4, 2, "V")
-        xt(4, 2)
-        xt(4, 3)
-        ee(2, 0)
-        xcp(4, 1, "S")
-        mxl(3, "g", 0)
-        nn(2, 0)
-        xcp(4, 2, "S")
-        mxl(3, "h", 0)
-        yy(1)
-        store(out_0, "y", 1, None)
-        xcp(4, 3, "S")
-        actl(3, "g", 0)
-        dd(2, 1)
-        actl(3, "h", 0)
-        pbias(2, 0)
-        mxl(3, "f", 0)
-        xr(5, 3, "S")
-        actl(3, "f", 0)
-        ee(2, 1)
-        pbias(2, 1)
-        nn(2, 1)
-        nt(2, 0)
-        nt(2, 1)
-        xt(5, 0)
-        mxl(3, "g", 1)
-        mxl(3, "h", 1)
-        ncp(2, 0, "S")
-        mxl(3, "f", 1)
-        ncp(2, 1, "S")
-        store(out_1, "nht", 2, None)
-        mxp(3, 0)
-        xcp(5, 0, "S")
-        xr(5, 1, "V")
-        xqz(4)
-        actl(3, "g", 1)
-        mxp(3, 1)
-        xt(5, 1)
-        actl(3, "h", 1)
-        dd(3, 0)
-        xr(6, 0, "S")
-        actl(3, "f", 1)
-        xr(5, 2, "V")
-        xt(5, 2)
-        xt(5, 3)
-        mxl(4, "g", 0)
-        mxl(4, "h", 0)
-        ee(3, 0)
-        xcp(5, 1, "S")
-        nn(3, 0)
-        xcp(5, 2, "S")
-        yy(2)
-        store(out_0, "y", 2, None)
-        xcp(5, 3, "S")
-        actl(4, "g", 0)
-        dd(3, 1)
-        actl(4, "h", 0)
-        pbias(3, 0)
-        mxl(4, "f", 0)
-        xr(6, 3, "S")
-        actl(4, "f", 0)
-        ee(3, 1)
-        pbias(3, 1)
-        nn(3, 1)
-        nt(3, 0)
-        nt(3, 1)
-        xt(6, 0)
-        mxl(4, "g", 1)
-        mxl(4, "h", 1)
-        mxl(4, "f", 1)
-        mxp(4, 0)
-        ncp(3, 0, "S")
-        ncp(3, 1, "S")
-        store(out_1, "nht", 3, None)
-        xcp(6, 0, "S")
-        xr(6, 1, "V")
-        xqz(5)
-        actl(4, "g", 1)
-        mxp(4, 1)
-        xt(6, 1)
-        actl(4, "h", 1)
-        dd(4, 0)
-        xr(7, 0, "S")
-        actl(4, "f", 1)
-        xr(6, 2, "V")
-        xt(6, 2)
-        xt(6, 3)
-        mxl(5, "g", 0)
-        mxl(5, "h", 0)
-        ee(4, 0)
-        xcp(6, 1, "S")
-        nn(4, 0)
-        xcp(6, 2, "S")
-        yy(3)
-        store(out_0, "y", 3, None)
-        xcp(6, 3, "S")
-        actl(5, "g", 0)
-        dd(4, 1)
-        actl(5, "h", 0)
-        pbias(4, 0)
-        mxl(5, "f", 0)
-        xr(7, 3, "S")
-        actl(5, "f", 0)
-        ee(4, 1)
-        pbias(4, 1)
-        nn(4, 1)
-        nt(4, 0)
-        nt(4, 1)
-        xt(7, 0)
-        mxl(5, "g", 1)
-        mxl(5, "h", 1)
-        mxl(5, "f", 1)
-        mxp(5, 0)
-        ncp(4, 0, "S")
-        ncp(4, 1, "S")
-        store(out_1, "nht", 4, None)
-        xcp(7, 0, "S")
-        xr(7, 1, "V")
-        xqz(6)
-        actl(5, "g", 1)
-        mxp(5, 1)
-        xt(7, 1)
-        actl(5, "h", 1)
-        dd(5, 0)
-        actl(5, "f", 1)
-        xr(7, 2, "V")
-        xt(7, 2)
-        xt(7, 3)
-        mxl(6, "g", 0)
-        mxl(6, "h", 0)
-        xcp(7, 1, "S")
-        ee(5, 0)
-        xcp(7, 2, "S")
-        nn(5, 0)
-        xcp(7, 3, "S")
-        yy(4)
-        store(out_0, "y", 4, None)
-        actl(6, "g", 0)
-        actl(6, "h", 0)
-        dd(5, 1)
-        pbias(5, 0)
-        mxl(6, "f", 0)
-        actl(6, "f", 0)
-        ee(5, 1)
-        pbias(5, 1)
-        nn(5, 1)
-        nt(5, 0)
-        nt(5, 1)
-        mxl(6, "g", 1)
-        mxl(6, "h", 1)
-        mxl(6, "f", 1)
-        mxp(6, 0)
-        ncp(5, 0, "S")
-        ncp(5, 1, "S")
-        store(out_1, "nht", 5, None)
-        actl(6, "g", 1)
-        mxp(6, 1)
-        actl(6, "h", 1)
-        xqz(7)
-        mxl(7, "g", 0)
-        actl(6, "f", 1)
-        mxl(7, "h", 0)
-        actl(7, "g", 0)
-        dd(6, 0)
-        actl(7, "h", 0)
-        ee(6, 0)
-        nn(6, 0)
-        yy(5)
-        store(out_0, "y", 5, None)
-        dd(6, 1)
-        pbias(6, 0)
-        mxl(7, "f", 0)
-        actl(7, "f", 0)
-        ee(6, 1)
-        pbias(6, 1)
-        nn(6, 1)
-        nt(6, 0)
-        nt(6, 1)
-        mxl(7, "g", 1)
-        mxl(7, "h", 1)
-        mxl(7, "f", 1)
-        mxp(7, 0)
-        ncp(6, 0, "S")
-        ncp(6, 1, "S")
-        store(out_1, "nht", 6, None)
-        actl(7, "g", 1)
-        mxp(7, 1)
-        actl(7, "h", 1)
-        actf2(7, 2)
-        actf2(7, 3)
-        dd(7, 0)
-        ee(7, 0)
-        yy(6)
-        store(out_0, "y", 6, None)
-        nn(7, 0)
-        dd(7, 1)
-        ee2(7, 2)
-        ee2(7, 3)
-        nn2(7, 2)
-        nt(7, 0)
-        ncp(7, 0, "S")
-        store(out_1, "nht", 7, 0)
-        nn2(7, 3)
-        nt(7, 1)
-        ncp(7, 1, "S")
-        store(out_1, "nht", 7, 1)
-        pbias(7, 0)
-        pbias(7, 1)
-        yh(7, 0)
-        yh(7, 1)
-        store(out_0, "y", 7, 0)
-        store(out_0, "y", 7, 1)
+
+        load_rows(0)
+        load_mask(0)
+        load_weight(0, 0)
+        load_mask(1)
+        load_weight(0, 1)
+        load_weight(1, 0)
+        load_weight(1, 1)
+        load_rows(1)
+        for w in range(2, 5):
+            for h in range(2):
+                load_weight(w, h)
+        for r in range(2, 6):
+            load_rows(r)
+
+        dummy_matmuls(8)
+        for j in (1, 3, 2, 0):
+            transpose_tile(0, j)
+        for j in (1, 2, 0, 3):
+            gather_tile(0, j, on_scalar)
+        mask_weight(0, 0)
+        mask_weight(0, 1)
+        mask_weight(1, 0)
+        dummy_matmuls(2)
+        quantize_rows(0)
+        transpose_weight(0, 1)
+        gather_weight(0, 1, on_scalar)
+        dummy_matmuls(2)
+        quantize_half(0, 1)
+        transpose_weight(1, 0)
+        gather_weight(1, 0, on_scalar)
+        transpose_weight(0, 0)
+        gather_weight(0, 0, on_scalar)
+        mask_weight(1, 1)
+        quantize_half(1, 0)
+        quantize_half(0, 0)
+        multiply(0, "g", 1)
+        transpose_weight(1, 1)
+        gather_weight(1, 1, on_scalar)
+        transpose_tile(1, 2)
+        gather_tile(1, 2, on_scalar)
+        transpose_tile(1, 3)
+        multiply(0, "g", 0)
+
+        mask_weight(2, 0)
+        prepare_biases()
+        gather_tile(1, 3, on_vector)
+        transpose_biases()
+        finish_biases()
+        activate(0, "g", 1)
+        spread_bp()
+        quantize_half(1, 1)
+        transpose_tile(1, 1)
+        transpose_tile(1, 0)
+        gather_tile(1, 0, on_scalar)
+        gather_tile(1, 1, on_scalar)
+        activate(0, "g", 0)
+        mask_weight(2, 1)
+        multiply(0, "h", 1)
+        multiply(0, "h", 0)
+        activate(0, "h", 0)
+        activate(0, "h", 1)
+
+        mask_weight(3, 1)
+        mask_weight(3, 0)
+        quantize_rows(1)
+        transpose_weight(2, 0)
+        gather_weight(2, 0, on_scalar)
+        transpose_weight(3, 1)
+        transpose_weight(3, 0)
+        gather_weight(3, 0, on_vector)
+        gather_weight(3, 1, on_vector)
+        transpose_weight(2, 1)
+        quantize_half(3, 0)
+        multiply(1, "g", 0)
+        activate(1, "g", 0)
+        gather_weight(2, 1, on_scalar)
+        quantize_half(3, 1)
+        quantize_half(2, 0)
+        multiply(1, "h", 1)
+        activate(1, "h", 1)
+        difference(0, 0)
+        multiply(1, "g", 1)
+        activate(1, "g", 1)
+        quantize_half(2, 1)
+        multiply(1, "h", 0)
+        activate(1, "h", 0)
+
+        mask_weight(4, 1)
+        mask_weight(4, 0)
+        multiply(0, "f", 0)
+        activate(0, "f", 0)
+        sort_words(2, 3, on_scalar)
+        difference(1, 0)
+        multiply(0, "f", 1)
+        weigh(0, 0)
+        transpose_weight(4, 0)
+        gather_weight(4, 0, on_scalar)
+        activate(0, "f", 1)
+        difference(0, 1)
+        transpose_weight(4, 1)
+        gather_weight(4, 1, on_scalar)
+        blend(0, 0)
+        transpose_tile(2, 0)
+        transpose_tile(2, 1)
+        gather_tile(2, 1, on_scalar)
+        gather_tile(2, 0, on_scalar)
+        multiply(1, "f", 0)
+        weigh(0, 1)
+        activate(1, "f", 0)
+        multiply(1, "f", 1)
+        difference(1, 1)
+        activate(1, "f", 1)
+        transpose_tile(2, 3)
+        blend(0, 1)
+        transpose_tile(2, 2)
+        gather_tile(2, 2, on_scalar)
+        gather_tile(2, 3, on_scalar)
+        quantize_wp()
+        transpose_back("new_hidden", 0, 1)
+        transpose_back("new_hidden", 0, 0)
+        transpose_bp()
+
+        weigh(1, 0)
+        weigh(1, 1)
+        sort_words(3, 0, on_scalar)
+        copy_hidden(0, 0)
+        copy_hidden(0, 1)
+        multiply_p(0, 0)
+        blend(1, 0)
+        multiply_p(1, 0)
+        multiply_p(1, 1)
+        sort_words(4, 0, on_scalar)
+        sort_words(4, 3, on_scalar)
+        sort_words(3, 2, on_vector)
+        finish_bp()
+        multiply_p(0, 1)
+        add_bp(0, 0)
+        for j in (1, 0, 2, 3):
+            transpose_tile(3, j)
+        quantize_rows(2)
+        for j in (0, 3, 1, 2):
+            gather_tile(3, j, on_scalar)
+        load_rows(6)
+        load_rows(7)
+        blend(1, 1)
+        add_bp(1, 0)
+        add_bp(0, 1)
+        add_bp(1, 1)
+        add_hidden(0)
+        store_round(0)
+
+
+        for r in range(2, 6):
+            multiply(r, "g", 0)
+            multiply(r, "h", 0)
+            multiply(r, "f", 0)
+            activate(r, "g", 0)
+            transpose_back("new_hidden", r - 1, 0)
+            transpose_back("new_hidden", r - 1, 1)
+            transpose_tile(r + 2, 0)
+            sort_words(r + 2, 1, on_vector)
+            quantize_rows(r + 1)
+            activate(r, "h", 0)
+            difference(r, 0)
+            if r > 2:
+                sort_words(r + 2, 3, on_scalar)
+            activate(r, "f", 0)
+            multiply(r, "g", 1)
+            multiply(r, "h", 1)
+            sort_words(r + 2, 2, on_vector)
+            weigh(r, 0)
+            copy_hidden(r - 1, 0)
+            multiply(r, "f", 1)
+            multiply_p(r, 0)
+            copy_hidden(r - 1, 1)
+            blend(r, 0)
+            gather_tile(r + 2, 0, on_scalar)
+            activate(r, "g", 1)
+            add_hidden(r - 1)
+            activate(r, "h", 1)
+            store_round(r - 1)
+            multiply_p(r, 1)
+            difference(r, 1)
+            transpose_tile(r + 2, 1)
+            if 2 < r < 5:
+                sort_words(r + 3, 0, on_scalar)
+            activate(r, "f", 1)
+            gather_tile(r + 2, 1, on_scalar)
+            transpose_tile(r + 2, 2)
+            add_bp(r, 0)
+            weigh(r, 1)
+            transpose_tile(r + 2, 3)
+            add_bp(r, 1)
+            gather_tile(r + 2, 2, on_scalar)
+            blend(r, 1)
+            gather_tile(r + 2, 3, on_scalar)
+
+
+        multiply(6, "g", 0)
+        multiply(6, "h", 0)
+        multiply(6, "f", 0)
+        activate(6, "g", 0)
+        transpose_back("new_hidden", 5, 0)
+        transpose_back("new_hidden", 5, 1)
+        quantize_rows(7)
+        activate(6, "h", 0)
+        difference(6, 0)
+        activate(6, "f", 0)
+        multiply(6, "g", 1)
+        multiply(6, "h", 1)
+        weigh(6, 0)
+        copy_hidden(5, 0)
+        multiply(6, "f", 1)
+        copy_hidden(5, 1)
+        blend(6, 0)
+        activate(6, "g", 1)
+        activate(6, "h", 1)
+        difference(6, 1)
+        activate(6, "f", 1)
+        weigh(6, 1)
+        blend(6, 1)
+        add_hidden(5)
+        store_round(5)
+
+        multiply(7, "h", 0)
+        multiply(7, "g", 0)
+        multiply(7, "f", 0)
+        activate(7, "h", 0)
+        activate(7, "g", 0)
+        multiply_p_features(6, 0)
+        multiply_p_features(6, 1)
+        activate(7, "f", 0)
+        difference(7, 0)
+        add_to_p_features(6, 0)
+        transpose_back("new_hidden", 6, 0)
+        transpose_back("new_hidden", 6, 1)
+        copy_hidden(6, 0)
+        copy_hidden(6, 1)
+        multiply(7, "g", 1)
+        multiply(7, "h", 1)
+        weigh(7, 0)
+        add_to_p_features(6, 1)
+        blend(7, 0)
+        activate(7, "g", 1)
+        activate(7, "h", 1)
+        multiply(7, "f", 1)
+        difference(7, 1)
+        transpose_back("y_features", 6, 0)
+        transpose_back("y_features", 6, 1)
+        early, late = slice(0, ROUND // 2), slice(ROUND // 2, ROUND)
+        for tokens in (early, late):
+            activate(7, "f", 1, tokens)
+        copy_y(6, 0)
+        copy_y(6, 1)
+        store_round(6)
+        for tokens in (early, late):
+            weigh(7, 1, tokens)
+        for tokens in (early, late):
+            blend(7, 1, tokens)
+        for p in range(2):
+            multiply_p(7, p)
+        for p in range(2):
+            transpose_back("new_hidden", 7, p)
+        for p in range(2):
+            add_bp(7, p)
+        for p in range(2):
+            copy_hidden(7, p)
+            store_pair(out_1, "hidden_rows", 7, p)
+        for p in range(2):
+            add_hidden_pair(7, p)
+            store_pair(out_0, "y_rows", 7, p)

from contextlib import ExitStack

import concourse.mybir as mybir
from concourse.masks import make_identity

F32 = mybir.dt.float32
BF16 = mybir.dt.bfloat16
U32 = mybir.dt.uint32
U8 = mybir.dt.uint8
FP8X4 = mybir.dt.float8_e4m3fn_x4
ALU = mybir.AluOpType
ACT = mybir.ActivationFunctionType

P = 128
TOKENS, IN_F, N_HID = 4096, 768, 256
K = IN_F + N_HID
ROUND = 512
TILES = ROUND // P
ROUNDS = TOKENS // ROUND
PASSES = K // 512
MX_ALIGN = 64
FLOPS = 2 * TOKENS * K * 5 * N_HID


def tile_ncpliquidcell_t_kernel(
    tc, x, hidden, mask, Wg, bg, Wh, bh, Wfg, bfg, Wfh, bfh, Wp, bp, out_0, out_1
):
    nc = tc.nc
    on_scalar, on_vector = nc.scalar.copy, nc.vector.tensor_copy
    weights = [Wg, Wh, Wfg, Wfh, Wp]
    WP = 4
    layers = {"g": [0], "h": [1], "f": [2, 3]}

    with ExitStack() as ctx:
        const = ctx.enter_context(tc.tile_pool(name="const", bufs=1))
        w_pool = ctx.enter_context(tc.tile_pool(name="w", bufs=10))
        w_grouped_pool = ctx.enter_context(tc.tile_pool(name="w_grouped", bufs=2))
        x_pool = ctx.enter_context(tc.tile_pool(name="x", bufs=ROUNDS - 2))
        sorted_pool = ctx.enter_context(tc.tile_pool(name="sorted", bufs=6))
        x_grouped_pool = ctx.enter_context(tc.tile_pool(name="x_grouped", bufs=2))
        x_codes_pool = ctx.enter_context(tc.tile_pool(name="x_codes", bufs=3))
        tanh_pool = ctx.enter_context(tc.tile_pool(name="tanh", bufs=3))
        blend_pool = ctx.enter_context(tc.tile_pool(name="blend", bufs=2))
        y_features_pool = ctx.enter_context(tc.tile_pool(name="y_features", bufs=1))
        out_pool = ctx.enter_context(tc.tile_pool(name="out", bufs=3))
        tr_pool = ctx.enter_context(tc.psum_pool(name="tr", bufs=4))
        mx_pool = ctx.enter_context(tc.psum_pool(name="mx", bufs=4))
        ctx.enter_context(tc.manual_schedule())

        ones = const.tile([P, P], BF16, name="ones")
        nc.vector.memset(ones[:], 1.0)
        zeros = const.tile([P, 512], BF16, name="zeros")
        nc.vector.memset(zeros[:], 0.0)
        bias_rows = const.tile([P, P], BF16, name="bias_rows")
        nc.vector.memset(bias_rows[:], 0.0)
        bp_row = const.tile([P, N_HID], BF16, name="bp_row")
        nc.vector.memset(bp_row[:], 0.0)
        zero_col = const.tile([P, 1], F32, name="zero_col")
        nc.vector.memset(zero_col[:], 0.0)
        tanh_col = const.tile([P, 1], F32, name="tanh_col")
        nc.scalar.activation(out=tanh_col[:], in_=zero_col[:], func=ACT.Tanh)
        identity = const.tile([P, P], F32, name="identity")
        make_identity(nc, identity[:])
        for i, b in enumerate([bg, bh, bfg, bfh]):
            nc.gpsimd.dma_start(out=bias_rows[2 * i : 2 * i + 2, :], in_=b.rearrange("(r c) -> r c", r=2))
        nc.gpsimd.dma_start(out=bp_row[0:1, :], in_=bp.rearrange("(o c) -> o c", o=1))

        mask_sb = [const.tile([P, K], BF16, name="mask%d" % h) for h in range(2)]
        w_sb = [[w_pool.tile([P, K], BF16, name="w%d_%d" % (w, h), tag="w") for h in range(2)] for w in range(5)]

        bias_words = const.tile([P, P], F32, name="bias_words")
        bias_cols = const.tile([P, 8], F32, name="bias_cols")
        gate_sum = const.tile([P, 2], F32, name="gate_sum")
        gate_bias = const.tile([P, 2], F32, name="gate_bias")
        bp_spread = const.tile([P, 2, N_HID], F32, name="bp_spread")
        bp_cols = const.tile([P, 2], F32, name="bp_cols")

        w_codes = [const.tile([P, 2, PASSES, P], U32, name="w_codes%d" % w, align_bytes=MX_ALIGN) for w in range(WP)]
        w_scales = [const.tile([P, 2, PASSES, P], U8, name="w_scales%d" % w, align_bytes=MX_ALIGN) for w in range(WP)]
        w_codes.append(const.tile([P, PASSES, N_HID], U32, name="w_codes4", align_bytes=MX_ALIGN))
        w_scales.append(const.tile([P, PASSES, N_HID], U8, name="w_scales4", align_bytes=MX_ALIGN))

        tiles = {}
        x_sb = {}


        def load_mask(h):
            nc.sync.dma_start(out=mask_sb[h][:], in_=mask[P * h : P * (h + 1), :])

        def load_weight(w, h):
            nc.sync.dma_start(out=w_sb[w][h][:], in_=weights[w][P * h : P * (h + 1), :])

        def load_rows(r):
            rows = slice(ROUND * r, ROUND * (r + 1))
            x_sb[r] = x_pool.tile([P, TILES, K], BF16, name="x_rows", tag="x")
            nc.sync.dma_start(out=x_sb[r][:, :, 0:IN_F], in_=x[rows, :].rearrange("(q j) k -> q j k", j=TILES))
            nc.sync.dma_start(out=x_sb[r][:, :, IN_F:K], in_=hidden[rows, :].rearrange("(q j) k -> q j k", j=TILES))


        def dummy_matmuls(count):
            if "dummy" not in tiles:
                tiles["dummy"] = mx_pool.tile([P, 512], F32, tag="mx", name="dummy")
            for i in range(count):
                nc.tensor.matmul(out=tiles["dummy"][:], lhsT=ones[:], rhs=zeros[:], start=True, stop=True)

        def prepare_biases():
            nc.vector.tensor_copy(out=bias_words[:], in_=bias_rows[:])

        def transpose_biases():
            bank = mx_pool.tile([P, 512], F32, tag="mx", name="bias_bank")
            tiles["bias"] = bank
            nc.tensor.transpose(bank[:, 0:P], bias_words[:], identity[:])
            nc.tensor.matmul(out=bank[:, P : P + N_HID], lhsT=ones[:], rhs=bp_row[:], start=True, stop=True)

        def finish_biases():
            nc.vector.tensor_copy(out=bias_cols[:], in_=tiles["bias"][:, 0:8])
            nc.vector.tensor_tensor(out=gate_sum[:], in0=bias_cols[:, 4:6], in1=bias_cols[:, 6:8], op=ALU.add)
            nc.vector.tensor_scalar_mul(out=gate_bias[:], in0=gate_sum[:], scalar1=0.5)

        def spread_bp():
            for i in range(2):
                on_scalar(out=bp_spread[:, i, :], in_=tiles["bias"][:, P : P + N_HID])

        def transpose_bp():
            tiles["bp"] = mx_pool.tile([P, 512], F32, tag="mx", name="bp_bank")
            for h in range(2):
                cols = slice(P * h, P * (h + 1))
                nc.tensor.transpose(tiles["bp"][:, cols], bp_spread[:, 0, cols], identity[:])

        def finish_bp():
            nc.vector.tensor_copy(out=bp_cols[:], in_=tiles["bp"][:, 0 : 2 * P : P])


        def transpose_words(words):
            bank = tr_pool.tile([P, 512], F32, tag="tr", name="words")
            for g in range(PASSES):
                for u in range(2):
                    o = P * (2 * g + u)
                    nc.tensor.transpose(bank[:, o : o + P], words(g, u), identity[:])
            return bank

        def every_second(row_words):
            return lambda g, u: row_words[:, 256 * g + u : 256 * (g + 1) : 2]

        def gather(copy, out, bank):
            copy(out=out, in_=bank[:].rearrange("q (g u c) -> q g c u", g=PASSES, u=2))


        def mask_weight(w, h):
            nc.vector.tensor_tensor(out=w_sb[w][h][:], in0=w_sb[w][h][:], in1=mask_sb[h][:], op=ALU.mult)

        def transpose_weight(w, h):
            tiles["w_words", w, h] = transpose_words(every_second(w_sb[w][h][:].bitcast(F32)))

        def gather_weight(w, h, copy):
            if ("w_grouped", w) not in tiles:
                tiles["w_grouped", w] = w_grouped_pool.tile(
                    [P, 2, PASSES, P, 2], F32, tag="w_grouped", name="w_grouped", align_bytes=MX_ALIGN
                )
            grouped = tiles["w_grouped", w]
            if w == WP:
                part = grouped[:].rearrange("q a b c u -> q a (b c) u")[:, :, P * h : P * (h + 1), :]
            else:
                part = grouped[:, h, :, :, :]
            gather(copy, part, tiles["w_words", w, h])

        def quantize_half(w, h):
            nc.vector.quantize_mx(
                out=w_codes[w][:, h, :, :].rearrange("q g c -> q (g c)").bitcast(FP8X4),
                scales=w_scales[w][:, h, :, :].rearrange("q g c -> q (g c)"),
                in_=tiles["w_grouped", w][:, h, :, :, :].rearrange("q g c u -> q (g c u)").bitcast(BF16),
            )

        def quantize_wp():
            nc.vector.quantize_mx(
                out=w_codes[WP][:].rearrange("q g c -> q (g c)").bitcast(FP8X4),
                scales=w_scales[WP][:].rearrange("q g c -> q (g c)"),
                in_=tiles["w_grouped", WP][:].rearrange("q a b c u -> q (a b c u)").bitcast(BF16),
            )


        def sort_words(r, j, copy):
            tiles["sorted", r, j] = sorted_pool.tile([P, PASSES, 2, P], F32, tag="sorted", name="sorted_words")
            copy(
                out=tiles["sorted", r, j][:],
                in_=x_sb[r][:, j, :].bitcast(F32).rearrange("q (g c u) -> q g u c", g=PASSES, u=2),
            )

        def transpose_tile(r, j):
            if ("sorted", r, j) in tiles:
                in_order = tiles["sorted", r, j]
                tiles["x_words", r, j] = transpose_words(lambda g, u: in_order[:, g, u, :])
            else:
                tiles["x_words", r, j] = transpose_words(every_second(x_sb[r][:, j, :].bitcast(F32)))

        def gather_tile(r, j, copy):
            if ("x_grouped", r) not in tiles:
                tiles["x_grouped", r] = x_grouped_pool.tile(
                    [P, PASSES, ROUND, 2], F32, tag="x_grouped", name="x_grouped", align_bytes=MX_ALIGN
                )
            gather(copy, tiles["x_grouped", r][:, :, P * j : P * (j + 1), :], tiles["x_words", r, j])

        def quantize_rows(r):
            tiles["x_codes", r] = x_codes_pool.tile([P, PASSES, ROUND], U32, tag="codes", name="x_codes", align_bytes=MX_ALIGN)
            tiles["x_scales", r] = x_codes_pool.tile([P, PASSES, ROUND], U8, tag="scales", name="x_scales", align_bytes=MX_ALIGN)
            nc.vector.quantize_mx(
                out=tiles["x_codes", r][:].rearrange("q g c -> q (g c)").bitcast(FP8X4),
                scales=tiles["x_scales", r][:].rearrange("q g c -> q (g c)"),
                in_=tiles["x_grouped", r][:].rearrange("q g c u -> q (g c u)").bitcast(BF16),
            )


        def add_up(bank, weight_views, r):
            passes = [(codes, scales, g) for codes, scales in weight_views for g in range(PASSES)]
            for i, (codes, scales, g) in enumerate(passes):
                nc.tensor.matmul_mx(
                    out=bank[:],
                    lhsT=codes(g).bitcast(FP8X4),
                    lhsT_scale=scales(g),
                    rhs=tiles["x_codes", r][:, g, :].bitcast(FP8X4),
                    rhs_scale=tiles["x_scales", r][:, g, :],
                    start=(i == 0),
                    stop=(i == len(passes) - 1),
                )

        def multiply(r, layer, h):
            bank = mx_pool.tile([P, 512], F32, tag="mx", name="layer")
            tiles[layer, r, h] = bank
            views = [
                (lambda g, w=w: w_codes[w][:, h, g, :], lambda g, w=w: w_scales[w][:, h, g, :]) for w in layers[layer]
            ]
            add_up(bank, views, r)

        def multiply_p_features(r, h):
            bank = mx_pool.tile([P, 512], F32, tag="mx", name="p_features")
            tiles["p_features", r, h] = bank
            cols = slice(P * h, P * (h + 1))
            add_up(bank, [(lambda g: w_codes[WP][:, g, cols], lambda g: w_scales[WP][:, g, cols])], r)

        def multiply_p(r, p):
            bank = mx_pool.tile([P, 512], F32, tag="mx", name="p_tokens")
            tiles["p", r, p] = bank
            for i in range(2):
                cols = slice(P * (2 * p + i), P * (2 * p + i + 1))
                for g in range(PASSES):
                    nc.tensor.matmul_mx(
                        out=bank[:, N_HID * i : N_HID * (i + 1)],
                        lhsT=tiles["x_codes", r][:, g, cols].bitcast(FP8X4),
                        lhsT_scale=tiles["x_scales", r][:, g, cols],
                        rhs=w_codes[WP][:, g, :].bitcast(FP8X4),
                        rhs_scale=w_scales[WP][:, g, :],
                        start=(g == 0),
                        stop=(g == PASSES - 1),
                    )


        def tile_of(pool, what, r, name):
            if (what, r) not in tiles:
                tiles[what, r] = pool.tile([P, 2, ROUND], F32, tag=what, name=name)
            return tiles[what, r]

        bias_of = {"g": (bias_cols, 0, 1.0), "h": (bias_cols, 2, 1.0), "f": (gate_bias, 0, 0.5)}
        every = slice(0, ROUND)

        def activate(r, layer, h, tokens=every):
            cols, first, scale = bias_of[layer]
            nc.scalar.activation(
                out=tile_of(tanh_pool, "tanh_" + layer, r, "tanh")[:, h, tokens],
                in_=tiles[layer, r, h][:, tokens],
                func=ACT.Tanh,
                bias=cols[:, first + h : first + h + 1],
                scale=scale,
            )

        def difference(r, h):
            nc.vector.tensor_tensor(
                out=tile_of(blend_pool, "step", r, "step")[:, h, :],
                in0=tiles["tanh_h", r][:, h, :],
                in1=tiles["tanh_g", r][:, h, :],
                op=ALU.subtract,
            )

        def weigh(r, h, tokens=every):
            step = tiles["step", r][:, h, tokens]
            nc.vector.scalar_tensor_tensor(
                out=step, in0=tiles["tanh_f", r][:, h, tokens], scalar=1.0, in1=step, op0=ALU.add, op1=ALU.mult
            )

        def blend(r, h, tokens=every):
            nc.vector.scalar_tensor_tensor(
                out=tile_of(blend_pool, "new_hidden", r, "new_hidden")[:, h, tokens],
                in0=tiles["step", r][:, h, tokens],
                scalar=0.5,
                in1=tiles["tanh_g", r][:, h, tokens],
                op0=ALU.mult,
                op1=ALU.add,
            )

        def add_to_p_features(r, h):
            nc.vector.scalar_tensor_tensor(
                out=tile_of(y_features_pool, "y_features", r, "y_features")[:, h, :],
                in0=tiles["p_features", r, h][:],
                scalar=bp_cols[:, h : h + 1],
                in1=tiles["new_hidden", r][:, h, :],
                op0=ALU.add,
                op1=ALU.add,
            )


        def rows_tile(what, r):
            if (what, r) not in tiles:
                tiles[what, r] = out_pool.tile([P, TILES, N_HID], F32, tag=what, name="rows")
            return tiles[what, r]

        def pair(rows, p):
            return rows[:, 2 * p : 2 * p + 2, :].rearrange("q a f -> q (a f)")

        def transpose_back(what, r, p):
            bank = tr_pool.tile([P, 512], F32, tag="tr", name="back")
            tiles[what + "_back", r, p] = bank
            for i in range(2):
                for h in range(2):
                    o = N_HID * i + P * h
                    j = 2 * p + i
                    nc.tensor.transpose(bank[:, o : o + P], tiles[what, r][:, h, P * j : P * (j + 1)], identity[:])

        def copy_hidden(r, p):
            on_scalar(out=pair(rows_tile("hidden_rows", r), p), in_=tiles["new_hidden_back", r, p][:])

        def copy_y(r, p):
            on_scalar(out=pair(rows_tile("y_rows", r), p), in_=tiles["y_features_back", r, p][:])

        def add_bp(r, p):
            nc.vector.tensor_tensor(
                out=pair(rows_tile("p_rows", r), p),
                in0=tiles["p", r, p][:],
                in1=bp_spread[:].rearrange("q a f -> q (a f)"),
                op=ALU.add,
            )

        def add_hidden(r):
            nc.vector.tensor_tensor(
                out=rows_tile("y_rows", r)[:], in0=tiles["hidden_rows", r][:], in1=tiles["p_rows", r][:], op=ALU.add
            )

        def add_hidden_pair(r, p):
            nc.vector.tensor_tensor(
                out=pair(rows_tile("y_rows", r), p),
                in0=pair(tiles["hidden_rows", r], p),
                in1=pair(tiles["p_rows", r], p),
                op=ALU.add,
            )

        def rows_of(dst, r):
            return dst[ROUND * r : ROUND * (r + 1), :].rearrange("(q j) f -> q j f", j=TILES)

        def store_round(r):
            nc.sync.dma_start(out=rows_of(out_1, r), in_=tiles["hidden_rows", r][:])
            nc.sync.dma_start(out=rows_of(out_0, r), in_=tiles["y_rows", r][:])

        def store_pair(dst, what, r, p):
            js = slice(2 * p, 2 * p + 2)
            nc.sync.dma_start(out=rows_of(dst, r)[:, js, :], in_=tiles[what, r][:, js, :])


        load_rows(0)
        load_mask(0)
        load_weight(0, 0)
        load_mask(1)
        load_weight(0, 1)
        load_weight(1, 0)
        load_weight(1, 1)
        load_rows(1)
        for w in range(2, 5):
            for h in range(2):
                load_weight(w, h)
        for r in range(2, 6):
            load_rows(r)

        dummy_matmuls(8)
        for j in (1, 3, 2, 0):
            transpose_tile(0, j)
        for j in (1, 2, 0, 3):
            gather_tile(0, j, on_scalar)
        mask_weight(0, 0)
        mask_weight(0, 1)
        mask_weight(1, 0)
        dummy_matmuls(2)
        quantize_rows(0)
        transpose_weight(0, 1)
        gather_weight(0, 1, on_scalar)
        dummy_matmuls(2)
        quantize_half(0, 1)
        transpose_weight(1, 0)
        gather_weight(1, 0, on_scalar)
        transpose_weight(0, 0)
        gather_weight(0, 0, on_scalar)
        mask_weight(1, 1)
        quantize_half(1, 0)
        quantize_half(0, 0)
        multiply(0, "g", 1)
        transpose_weight(1, 1)
        gather_weight(1, 1, on_scalar)
        transpose_tile(1, 2)
        gather_tile(1, 2, on_scalar)
        transpose_tile(1, 3)
        multiply(0, "g", 0)

        mask_weight(2, 0)
        prepare_biases()
        gather_tile(1, 3, on_vector)
        transpose_biases()
        finish_biases()
        activate(0, "g", 1)
        spread_bp()
        quantize_half(1, 1)
        transpose_tile(1, 1)
        transpose_tile(1, 0)
        gather_tile(1, 0, on_scalar)
        gather_tile(1, 1, on_scalar)
        activate(0, "g", 0)
        mask_weight(2, 1)
        multiply(0, "h", 1)
        multiply(0, "h", 0)
        activate(0, "h", 0)
        activate(0, "h", 1)

        mask_weight(3, 1)
        mask_weight(3, 0)
        quantize_rows(1)
        transpose_weight(2, 0)
        gather_weight(2, 0, on_scalar)
        transpose_weight(3, 1)
        transpose_weight(3, 0)
        gather_weight(3, 0, on_vector)
        gather_weight(3, 1, on_vector)
        transpose_weight(2, 1)
        quantize_half(3, 0)
        multiply(1, "g", 0)
        activate(1, "g", 0)
        gather_weight(2, 1, on_scalar)
        quantize_half(3, 1)
        quantize_half(2, 0)
        multiply(1, "h", 1)
        activate(1, "h", 1)
        difference(0, 0)
        multiply(1, "g", 1)
        activate(1, "g", 1)
        quantize_half(2, 1)
        multiply(1, "h", 0)
        activate(1, "h", 0)

        mask_weight(4, 1)
        mask_weight(4, 0)
        multiply(0, "f", 0)
        activate(0, "f", 0)
        sort_words(2, 3, on_scalar)
        difference(1, 0)
        multiply(0, "f", 1)
        weigh(0, 0)
        transpose_weight(4, 0)
        gather_weight(4, 0, on_scalar)
        activate(0, "f", 1)
        difference(0, 1)
        transpose_weight(4, 1)
        gather_weight(4, 1, on_scalar)
        blend(0, 0)
        transpose_tile(2, 0)
        transpose_tile(2, 1)
        gather_tile(2, 1, on_scalar)
        gather_tile(2, 0, on_scalar)
        multiply(1, "f", 0)
        weigh(0, 1)
        activate(1, "f", 0)
        multiply(1, "f", 1)
        difference(1, 1)
        activate(1, "f", 1)
        transpose_tile(2, 3)
        blend(0, 1)
        transpose_tile(2, 2)
        gather_tile(2, 2, on_scalar)
        gather_tile(2, 3, on_scalar)
        quantize_wp()
        transpose_back("new_hidden", 0, 1)
        transpose_back("new_hidden", 0, 0)
        transpose_bp()

        weigh(1, 0)
        weigh(1, 1)
        sort_words(3, 0, on_scalar)
        copy_hidden(0, 0)
        copy_hidden(0, 1)
        multiply_p(0, 0)
        blend(1, 0)
        multiply_p(1, 0)
        multiply_p(1, 1)
        sort_words(4, 0, on_scalar)
        sort_words(4, 3, on_scalar)
        sort_words(3, 2, on_vector)
        finish_bp()
        multiply_p(0, 1)
        add_bp(0, 0)
        for j in (1, 0, 2, 3):
            transpose_tile(3, j)
        quantize_rows(2)
        for j in (0, 3, 1, 2):
            gather_tile(3, j, on_scalar)
        load_rows(6)
        load_rows(7)
        blend(1, 1)
        add_bp(1, 0)
        add_bp(0, 1)
        add_bp(1, 1)
        add_hidden(0)
        store_round(0)


        for r in range(2, 6):
            multiply(r, "g", 0)
            multiply(r, "h", 0)
            multiply(r, "f", 0)
            activate(r, "g", 0)
            transpose_back("new_hidden", r - 1, 0)
            transpose_back("new_hidden", r - 1, 1)
            transpose_tile(r + 2, 0)
            sort_words(r + 2, 1, on_vector)
            quantize_rows(r + 1)
            activate(r, "h", 0)
            difference(r, 0)
            if r > 2:
                sort_words(r + 2, 3, on_scalar)
            activate(r, "f", 0)
            multiply(r, "g", 1)
            multiply(r, "h", 1)
            sort_words(r + 2, 2, on_vector)
            weigh(r, 0)
            copy_hidden(r - 1, 0)
            multiply(r, "f", 1)
            multiply_p(r, 0)
            copy_hidden(r - 1, 1)
            blend(r, 0)
            gather_tile(r + 2, 0, on_scalar)
            activate(r, "g", 1)
            add_hidden(r - 1)
            activate(r, "h", 1)
            store_round(r - 1)
            multiply_p(r, 1)
            difference(r, 1)
            transpose_tile(r + 2, 1)
            if 2 < r < 5:
                sort_words(r + 3, 0, on_scalar)
            activate(r, "f", 1)
            gather_tile(r + 2, 1, on_scalar)
            transpose_tile(r + 2, 2)
            add_bp(r, 0)
            weigh(r, 1)
            transpose_tile(r + 2, 3)
            add_bp(r, 1)
            gather_tile(r + 2, 2, on_scalar)
            blend(r, 1)
            gather_tile(r + 2, 3, on_scalar)


        multiply(6, "g", 0)
        multiply(6, "h", 0)
        multiply(6, "f", 0)
        activate(6, "g", 0)
        transpose_back("new_hidden", 5, 0)
        transpose_back("new_hidden", 5, 1)
        quantize_rows(7)
        activate(6, "h", 0)
        difference(6, 0)
        activate(6, "f", 0)
        multiply(6, "g", 1)
        multiply(6, "h", 1)
        weigh(6, 0)
        copy_hidden(5, 0)
        multiply(6, "f", 1)
        copy_hidden(5, 1)
        blend(6, 0)
        activate(6, "g", 1)
        activate(6, "h", 1)
        difference(6, 1)
        activate(6, "f", 1)
        weigh(6, 1)
        blend(6, 1)
        add_hidden(5)
        store_round(5)

        multiply(7, "h", 0)
        multiply(7, "g", 0)
        multiply(7, "f", 0)
        activate(7, "h", 0)
        activate(7, "g", 0)
        multiply_p_features(6, 0)
        multiply_p_features(6, 1)
        activate(7, "f", 0)
        difference(7, 0)
        add_to_p_features(6, 0)
        transpose_back("new_hidden", 6, 0)
        transpose_back("new_hidden", 6, 1)
        copy_hidden(6, 0)
        copy_hidden(6, 1)
        multiply(7, "g", 1)
        multiply(7, "h", 1)
        weigh(7, 0)
        add_to_p_features(6, 1)
        blend(7, 0)
        activate(7, "g", 1)
        activate(7, "h", 1)
        multiply(7, "f", 1)
        difference(7, 1)
        transpose_back("y_features", 6, 0)
        transpose_back("y_features", 6, 1)
        early, late = slice(0, ROUND // 2), slice(ROUND // 2, ROUND)
        for tokens in (early, late):
            activate(7, "f", 1, tokens)
        copy_y(6, 0)
        copy_y(6, 1)
        store_round(6)
        for tokens in (early, late):
            weigh(7, 1, tokens)
        for tokens in (early, late):
            blend(7, 1, tokens)
        for p in range(2):
            multiply_p(7, p)
        for p in range(2):
            transpose_back("new_hidden", 7, p)
        for p in range(2):
            add_bp(7, p)
        for p in range(2):
            copy_hidden(7, p)
            store_pair(out_1, "hidden_rows", 7, p)
        for p in range(2):
            add_hidden_pair(7, p)
            store_pair(out_0, "y_rows", 7, p)
